import numpy as np
import ml_dtypes


def mxq(x, axis, fmt="e4m3"):
    dtype, down = {"e4m3": (ml_dtypes.float8_e4m3fn, 7), "e5m2": (ml_dtypes.float8_e5m2, 14)}[fmt]
    v = np.moveaxis(np.asarray(x, np.float32).astype(ml_dtypes.bfloat16).astype(np.float64), axis, -1)
    blocks = v.reshape(v.shape[:-1] + (-1, 32))
    amax = np.abs(blocks).max(-1, keepdims=True)
    byte = np.maximum(np.where(amax > 0, np.frexp(amax)[1] - 1 + 127, 0) - down, 1)
    scale = np.exp2(byte - 127.0)
    codes = (blocks / scale).astype(np.float32).astype(dtype).astype(np.float64)
    return np.moveaxis((codes * scale).reshape(v.shape), -1, axis)


BF16 = ml_dtypes.bfloat16


def bf(x):
    return np.asarray(x, np.float32).astype(BF16)


def f64(x):
    return np.asarray(x).astype(np.float64)


E2M1 = np.array([0.0, 0.5, 1.0, 1.5, 2.0, 3.0, 4.0, 6.0, -0.0, -0.5, -1.0, -1.5, -2.0, -3.0, -4.0, -6.0])


def pack_weight(w, fmt):
    k, n = w.shape
    w = f64(bf(w)).reshape(k // 32, 32, n)
    amax = np.abs(w).max(1)
    if fmt == "e4m3":
        byte = np.frexp(amax)[1] - 1 + 127 - 7
    else:
        mant, ex = np.frexp(amax / 6.0)
        byte = np.where(mant > 0.5, ex, ex - 1) + 127
    byte = np.clip(np.where(amax > 0, byte, 1), 1, 254)
    scaled = (w * np.exp2(127.0 - byte)[:, None, :]).reshape(k, n).astype(np.float32)
    by_word = np.ascontiguousarray(scaled.reshape(k // 512, 128, 4, n).transpose(0, 1, 3, 2))
    if fmt == "e4m3":
        words = by_word.astype(ml_dtypes.float8_e4m3fn).view(np.uint8)
    else:
        c = by_word.astype(ml_dtypes.float4_e2m1fn).view(np.uint8) & 0xF
        words = c[..., 0::2] | (c[..., 1::2] << 4)
    return np.ascontiguousarray(words), np.ascontiguousarray(byte.astype(np.uint8).reshape(k // 512, 16, n))


def unpack_weight(words, scales, fmt):
    g, p, n, _ = words.shape
    if fmt == "e4m3":
        vals = np.ascontiguousarray(words).view(ml_dtypes.float8_e4m3fn).astype(np.float64)
    else:
        nib = np.empty((g, p, n, 4), np.uint8)
        nib[..., 0::2] = words & 0xF
        nib[..., 1::2] = words >> 4
        vals = E2M1[nib]
    vals = vals * np.repeat(np.exp2(scales.astype(np.float64) - 127.0), 8, axis=1)[..., None]
    return vals.transpose(0, 1, 3, 2).reshape(g * 512, n)


C, H, N, L = 1, 512, 4096, 2048


def setup_inputs():
    stack = (np.random.standard_normal((C, H, N)) / np.sqrt(N)).swapaxes(1, 2)
    words, scales = pack_weight(stack.reshape(-1, H), "e4m3")
    return {"W_words": words, "W_scales": scales, "Lambda_im": bf(np.random.uniform(0.0, 2.0 * np.pi, N)), "L": L}


def reference(W_words, W_scales, Lambda_im, L):
    pos = np.arange(L, dtype=np.float64)
    S = np.cos(f64(Lambda_im)[:, None] * pos[None, :])
    return unpack_weight(W_words, W_scales, "e4m3").reshape(C, N, H).swapaxes(1, 2) @ mxq(S, 0, "e4m3")

@@ -1,0 +1,264 @@
+import math
+from contextlib import ExitStack
+
+import concourse.mybir as mybir
+
+FLOPS = 2 * 512 * 4096 * 2048
+
+F32 = mybir.dt.float32
+BF16 = mybir.dt.bfloat16
+I32 = mybir.dt.int32
+U32 = mybir.dt.uint32
+U8 = mybir.dt.uint8
+FP8X4 = mybir.dt.float8_e4m3fn_x4
+ALU = mybir.AluOpType
+
+P = 128
+PACK = 4
+GROUPS = 8
+PLANES = GROUPS * PACK
+H = 512
+H_TILES = H // P
+COLUMNS = 2048
+HALF = COLUMNS // 2
+CHUNK = 512
+CHUNKS = HALF // CHUNK
+CENTRE = HALF // 2
+SEED = 64
+LOWER_STEPS = (32, 64, 128, 256)
+UPPER_STEP = 512
+STEPS = LOWER_STEPS + (UPPER_STEP,)
+ARGS = len(STEPS) + SEED
+RUN = 4
+
+ROUND = 12582912.0
+INV_2PI_A = 41722.0 * 2.0**-18
+INV_2PI_B = -63779.0 * 2.0**-35
+INV_2PI_C = -13037483.0 * 2.0**-60
+GRID = 4096.0
+
+
+def turns_per_position(nc, pool, lam_bf):
+    names = ("lam", "lead", "whole", "lead_part", "turns", "shifted", "coarse", "rest", "fine")
+    lam, lead, whole, lead_part, turns, shifted, coarse, rest, fine = (
+        pool.tile([P, PLANES], F32, name=name) for name in names
+    )
+    nc.vector.tensor_copy(out=lam[:], in_=lam_bf[:].rearrange("p g t -> p (g t)"))
+    nc.vector.tensor_scalar(out=lead[:], in0=lam[:], scalar1=INV_2PI_A, scalar2=None, op0=ALU.mult)
+    nc.vector.tensor_scalar(
+        out=whole[:], in0=lead[:], scalar1=ROUND, scalar2=ROUND, op0=ALU.add, op1=ALU.subtract
+    )
+    nc.vector.tensor_tensor(out=lead_part[:], in0=lead[:], in1=whole[:], op=ALU.subtract)
+    nc.vector.scalar_tensor_tensor(
+        out=turns[:], in0=lam[:], scalar=INV_2PI_B, in1=lead_part[:], op0=ALU.mult, op1=ALU.add
+    )
+    nc.vector.tensor_scalar(
+        out=shifted[:], in0=turns[:], scalar1=GRID, scalar2=ROUND, op0=ALU.mult, op1=ALU.add
+    )
+    nc.vector.tensor_scalar(
+        out=coarse[:], in0=shifted[:], scalar1=ROUND, scalar2=1.0 / GRID, op0=ALU.subtract, op1=ALU.mult
+    )
+    nc.vector.tensor_tensor(out=rest[:], in0=lead_part[:], in1=coarse[:], op=ALU.subtract)
+    nc.vector.scalar_tensor_tensor(
+        out=rest[:], in0=lam[:], scalar=INV_2PI_B, in1=rest[:], op0=ALU.mult, op1=ALU.add
+    )
+    nc.vector.scalar_tensor_tensor(
+        out=fine[:], in0=lam[:], scalar=INV_2PI_C, in1=rest[:], op0=ALU.mult, op1=ALU.add
+    )
+    return coarse, fine
+
+
+def by_runs_of_planes(planes):
+    return planes.rearrange("p t (c i) -> p c t i", i=RUN)
+
+
+def by_runs_interleaved(grouped):
+    return grouped.rearrange("p (c i t) -> p c t i", i=RUN, t=PACK)
+
+
+def tile_dlrkernel_e_kernel(tc, W_words, W_scales, Lambda_im, L, out):
+    nc = tc.nc
+    assert L == COLUMNS
+    with ExitStack() as stack:
+        stack.enter_context(tc.manual_schedule())
+        keep = stack.enter_context(tc.tile_pool(name="keep", bufs=1))
+        stream = stack.enter_context(tc.tile_pool(name="stream", bufs=4))
+        banks = stack.enter_context(tc.psum_pool(name="banks", bufs=1))
+
+        lam_bf = keep.tile([P, GROUPS, PACK], BF16)
+        nc.sync.dma_start(out=lam_bf[:], in_=Lambda_im.rearrange("(g p t) -> p g t", p=P, t=PACK))
+        w_scales = keep.tile([P, GROUPS, H], U8, align_bytes=64)
+        nc.vector.memset(w_scales[:].rearrange("p g h -> p (g h)").bitcast(I32), 0)
+        for quadrant in range(4):
+            nc.sync.dma_start(
+                out=w_scales[32 * quadrant : 32 * quadrant + 4].bitcast(I32),
+                in_=W_scales[:, 4 * quadrant : 4 * quadrant + 4, :].rearrange("g q h -> q g h").bitcast(I32),
+            )
+        w_words = keep.tile([P, GROUPS, H * PACK], U8, align_bytes=64)
+        nc.sync.dma_start(
+            out=w_words[:].bitcast(I32), in_=W_words.rearrange("g p h t -> p g (h t)").bitcast(I32)
+        )
+
+        args = keep.tile([P, ARGS], F32)
+        for k, step in enumerate(STEPS):
+            nc.vector.memset(args[:, k : k + 1], float(step))
+        seed_positions = keep.tile([P, SEED], I32)
+        nc.gpsimd.iota(seed_positions[:], pattern=[[1, SEED]], base=CENTRE - SEED // 2, channel_multiplier=0)
+        nc.vector.tensor_copy(out=args[:, len(STEPS) :], in_=seed_positions[:])
+
+        coarse, fine = turns_per_position(nc, keep, lam_bf)
+
+        lower = [keep.tile([P, PACK, HALF], F32, name="lower%d" % g) for g in range(GROUPS)]
+        twice_cos = keep.tile([P, PLANES, len(STEPS)], F32)
+
+        with tc.tile_pool(name="seed_work", bufs=1) as work:
+            shape = [P, PLANES, ARGS]
+            args_of_all = args[:].unsqueeze(1).to_broadcast(shape)
+            turn = work.tile(shape, F32)
+            other = work.tile(shape, F32)
+            nc.vector.tensor_tensor(
+                out=turn[:], in0=args_of_all, in1=coarse[:].unsqueeze(2).to_broadcast(shape), op=ALU.mult
+            )
+            nc.vector.tensor_scalar(
+                out=other[:], in0=turn[:], scalar1=ROUND, scalar2=ROUND, op0=ALU.add, op1=ALU.subtract
+            )
+            nc.vector.tensor_tensor(out=turn[:], in0=turn[:], in1=other[:], op=ALU.subtract)
+            nc.vector.tensor_tensor(
+                out=other[:], in0=args_of_all, in1=fine[:].unsqueeze(2).to_broadcast(shape), op=ALU.mult
+            )
+            nc.vector.tensor_tensor(out=turn[:], in0=turn[:], in1=other[:], op=ALU.add)
+            nc.vector.scalar_tensor_tensor(
+                out=other[:], in0=turn[:], scalar=-1.0, in1=turn[:], op0=ALU.mult, op1=ALU.max
+            )
+            cos_step = work.tile([P, PLANES, len(STEPS)], F32)
+            nc.scalar.activation(
+                out=cos_step[:],
+                in_=other[:, :, : len(STEPS)],
+                func=mybir.ActivationFunctionType.Sin,
+                bias=math.pi / 2,
+                scale=-2.0 * math.pi,
+            )
+            nc.vector.tensor_scalar(out=twice_cos[:], in0=cos_step[:], scalar1=2.0, scalar2=None, op0=ALU.mult)
+            for g in range(GROUPS):
+                nc.scalar.activation(
+                    out=lower[g][:, :, CENTRE - SEED // 2 : CENTRE + SEED // 2],
+                    in_=other[:, PACK * g : PACK * (g + 1), len(STEPS) :],
+                    func=mybir.ActivationFunctionType.Sin,
+                    bias=math.pi / 2,
+                    scale=-2.0 * math.pi,
+                )
+
+        upper = stack.enter_context(tc.tile_pool(name="upper", bufs=2))
+
+        def next_columns(out_columns, middle, scale, far):
+            nc.vector.scalar_tensor_tensor(
+                out=out_columns, in0=middle, scalar=scale, in1=far, op0=ALU.mult, op1=ALU.subtract
+            )
+
+        def grow_lower_half(g):
+            for k, step in enumerate(LOWER_STEPS):
+                for t in range(PACK):
+                    plane = lower[g][:, t, :]
+                    scale = twice_cos[:, PACK * g + t, k : k + 1]
+                    left = plane[:, CENTRE - step : CENTRE]
+                    right = plane[:, CENTRE : CENTRE + step]
+                    next_columns(plane[:, CENTRE + step : CENTRE + 2 * step], right, scale, left)
+                    next_columns(plane[:, CENTRE - 2 * step : CENTRE - step], left, scale, right)
+
+        def odd_upper_columns(g):
+            odd = [upper.tile([P, PACK, CHUNK // 2], F32, name="odd%d" % c) for c in range(CHUNKS)]
+            for c in range(CHUNKS):
+                for t in range(PACK):
+                    scale = twice_cos[:, PACK * g + t, len(LOWER_STEPS) : len(STEPS)]
+                    low_odd = lower[g][:, t, 1:CENTRE:2]
+                    high_odd = lower[g][:, t, CENTRE + 1 : HALF : 2]
+                    if c == 0:
+                        next_columns(odd[0][:, t, :], high_odd, scale, low_odd)
+                    else:
+                        next_columns(odd[1][:, t, :], odd[0][:, t, :], scale, high_odd)
+            return odd
+
+        def squares_for_even_upper_columns(g):
+            square = [upper.tile([P, PACK * CHUNK // 2], F32, name="square%d" % c) for c in range(CHUNKS)]
+            for c in range(CHUNKS):
+                first = CENTRE + c * CHUNK // 2
+                nc.scalar.square(
+                    out=by_runs_interleaved(square[c][:]),
+                    in_=by_runs_of_planes(lower[g][:, :, first : first + CHUNK // 2]),
+                )
+            return square
+
+        def quantise_and_multiply(g, grouped, sums):
+            codes = stream.tile([P, CHUNK], U32, align_bytes=64)
+            scales = stream.tile([P, CHUNK], U8, align_bytes=64)
+            nc.vector.quantize_mx(out=codes[:].bitcast(FP8X4), scales=scales[:], in_=grouped[:])
+            for h in range(H_TILES):
+                nc.tensor.matmul_mx(
+                    out=sums[h][:],
+                    lhsT=w_words[:, g, P * PACK * h : P * PACK * (h + 1)].bitcast(FP8X4),
+                    lhsT_scale=w_scales[:, g, P * h : P * (h + 1)],
+                    rhs=codes[:].bitcast(FP8X4),
+                    rhs_scale=scales[:],
+                    start=(g == 0),
+                    stop=(g == GROUPS - 1),
+                )
+
+        def open_banks():
+            return [
+                [banks.tile([P, CHUNK], F32, name="sum%d%d" % (c, h)) for h in range(H_TILES)]
+                for c in range(CHUNKS)
+            ]
+
+        def store_half(half, sums, in_order):
+            for h in range(H_TILES):
+                result = stream.tile([P, HALF], F32, name="result")
+                for c, copy in enumerate((nc.scalar.copy, nc.vector.tensor_copy)):
+                    copy(
+                        out=in_order(result[:, CHUNK * c : CHUNK * (c + 1)]),
+                        in_=sums[c][h][:] if half == 0 else sums[c][h][:].rearrange("p (e r) -> p r e", e=2),
+                    )
+                nc.sync.dma_start(
+                    out=out[0, P * h : P * (h + 1), HALF * half : HALF * (half + 1)], in_=result[:]
+                )
+
+        sums = open_banks()
+        grow_lower_half(0)
+        for g in range(GROUPS):
+            grouped = [stream.tile([P, PACK * CHUNK], BF16, name="grouped", align_bytes=64) for c in range(CHUNKS)]
+            for c in range(CHUNKS):
+                nc.scalar.copy(
+                    out=by_runs_interleaved(grouped[c][:]),
+                    in_=by_runs_of_planes(lower[g][:, :, CHUNK * c : CHUNK * (c + 1)]),
+                )
+            if g + 1 < GROUPS:
+                grow_lower_half(g + 1)
+            else:
+                square = squares_for_even_upper_columns(0)
+                odd = odd_upper_columns(0)
+            for c in range(CHUNKS):
+                quantise_and_multiply(g, grouped[c], sums[c])
+        store_half(0, sums, lambda columns: columns)
+
+        sums = open_banks()
+        for g in range(GROUPS):
+            grouped = [stream.tile([P, PACK * CHUNK], BF16, name="grouped", align_bytes=64) for c in range(CHUNKS)]
+            for c in range(CHUNKS):
+                nc.scalar.copy(
+                    out=by_runs_interleaved(grouped[c][:, PACK * CHUNK // 2 :]), in_=by_runs_of_planes(odd[c][:])
+                )
+            this_square = square
+            if g + 1 < GROUPS:
+                square = squares_for_even_upper_columns(g + 1)
+                odd = odd_upper_columns(g + 1)
+            for c in range(CHUNKS):
+                nc.vector.tensor_scalar(
+                    out=grouped[c][:, : PACK * CHUNK // 2],
+                    in0=this_square[c][:],
+                    scalar1=2.0,
+                    scalar2=1.0,
+                    op0=ALU.mult,
+                    op1=ALU.subtract,
+                )
+            for c in range(CHUNKS):
+                quantise_and_multiply(g, grouped[c], sums[c])
+        store_half(1, sums, lambda columns: columns.rearrange("p (r e) -> p r e", e=2))

@@ -24,8 +24,8 @@ HALF = COLUMNS // 2
 CHUNK = 512
 CHUNKS = HALF // CHUNK
 CENTRE = HALF // 2
-SEED = 64
-LOWER_STEPS = (32, 64, 128, 256)
+SEED = 32
+LOWER_STEPS = (16, 32, 64, 128, 256)
 UPPER_STEP = 512
 STEPS = LOWER_STEPS + (UPPER_STEP,)
 ARGS = len(STEPS) + SEED
@@ -158,12 +158,15 @@ def tile_dlrkernel_e_kernel(tc, W_words, W_scales, Lambda_im, L, out):
         def grow_lower_half(g):
             for k, step in enumerate(LOWER_STEPS):
                 for t in range(PACK):
-                    plane = lower[g][:, t, :]
-                    scale = twice_cos[:, PACK * g + t, k : k + 1]
-                    left = plane[:, CENTRE - step : CENTRE]
-                    right = plane[:, CENTRE : CENTRE + step]
-                    next_columns(plane[:, CENTRE + step : CENTRE + 2 * step], right, scale, left)
-                    next_columns(plane[:, CENTRE - 2 * step : CENTRE - step], left, scale, right)
+                    blocks = lower[g][:, t, CENTRE - 2 * step : CENTRE + 2 * step].rearrange(
+                        "p (b j) -> p b j", b=4
+                    )
+                    next_columns(
+                        blocks[:, 0:4:3, :],
+                        blocks[:, 1:3, :],
+                        twice_cos[:, PACK * g + t, k : k + 1],
+                        blocks[:, 2:0:-1, :],
+                    )
 
         def odd_upper_columns(g):
             odd = [upper.tile([P, PACK, CHUNK // 2], F32, name="odd%d" % c) for c in range(CHUNKS)]
@@ -209,17 +212,17 @@ def tile_dlrkernel_e_kernel(tc, W_words, W_scales, Lambda_im, L, out):
                 for c in range(CHUNKS)
             ]
 
-        def store_half(half, sums, in_order):
-            for h in range(H_TILES):
-                result = stream.tile([P, HALF], F32, name="result")
-                for c, copy in enumerate((nc.scalar.copy, nc.vector.tensor_copy)):
+        def store_half(first_column, sums, strands):
+            for c in range(CHUNKS):
+                for h in range(H_TILES):
+                    result = stream.tile([P, CHUNK], F32, name="result", bufs=CHUNKS * H_TILES)
+                    copy = nc.scalar.copy if (c + h) % 2 == 0 else nc.vector.tensor_copy
                     copy(
-                        out=in_order(result[:, CHUNK * c : CHUNK * (c + 1)]),
-                        in_=sums[c][h][:] if half == 0 else sums[c][h][:].rearrange("p (e r) -> p r e", e=2),
+                        out=result[:].rearrange("p (r e) -> p r e", e=strands),
+                        in_=sums[c][h][:].rearrange("p (e r) -> p r e", e=strands),
                     )
-                nc.sync.dma_start(
-                    out=out[0, P * h : P * (h + 1), HALF * half : HALF * (half + 1)], in_=result[:]
-                )
+                    columns = first_column + CHUNK * c
+                    nc.sync.dma_start(out=out[0, P * h : P * (h + 1), columns : columns + CHUNK], in_=result[:])
 
         sums = open_banks()
         grow_lower_half(0)
@@ -237,9 +240,7 @@ def tile_dlrkernel_e_kernel(tc, W_words, W_scales, Lambda_im, L, out):
                 odd = odd_upper_columns(0)
             for c in range(CHUNKS):
                 quantise_and_multiply(g, grouped[c], sums[c])
-        store_half(0, sums, lambda columns: columns)
 
-        sums = open_banks()
         for g in range(GROUPS):
             grouped = [stream.tile([P, PACK * CHUNK], BF16, name="grouped", align_bytes=64) for c in range(CHUNKS)]
             for c in range(CHUNKS):
@@ -259,6 +260,9 @@ def tile_dlrkernel_e_kernel(tc, W_words, W_scales, Lambda_im, L, out):
                     op0=ALU.mult,
                     op1=ALU.subtract,
                 )
+            if g == 0:
+                store_half(0, sums, 1)
+                sums = open_banks()
             for c in range(CHUNKS):
                 quantise_and_multiply(g, grouped[c], sums[c])
-        store_half(1, sums, lambda columns: columns.rearrange("p (r e) -> p r e", e=2))
+        store_half(HALF, sums, 2)

@@ -12,6 +12,7 @@ U32 = mybir.dt.uint32
 U8 = mybir.dt.uint8
 FP8X4 = mybir.dt.float8_e4m3fn_x4
 ALU = mybir.AluOpType
+SIN = mybir.ActivationFunctionType.Sin
 
 P = 128
 PACK = 4
@@ -23,13 +24,13 @@ COLUMNS = 2048
 HALF = COLUMNS // 2
 CHUNK = 512
 CHUNKS = HALF // CHUNK
-CENTRE = HALF // 2
-SEED = 32
-LOWER_STEPS = (16, 32, 64, 128, 256)
-UPPER_STEP = 512
-STEPS = LOWER_STEPS + (UPPER_STEP,)
-ARGS = len(STEPS) + SEED
 RUN = 4
+PLANE = HALF + RUN
+SEED = 16
+STEPS = (16, 32, 64, 128, 256, 512, 1024)
+SHORT_STEPS = 2
+LOWER_STEPS = len(STEPS) - 1
+ARGS = len(STEPS) + SEED + 1
 
 ROUND = 12582912.0
 INV_2PI_A = 41722.0 * 2.0**-18
@@ -38,20 +39,21 @@ INV_2PI_C = -13037483.0 * 2.0**-60
 GRID = 4096.0
 
 
-def turns_per_position(nc, pool, lam_bf):
-    names = ("lam", "lead", "whole", "lead_part", "turns", "shifted", "coarse", "rest", "fine")
-    lam, lead, whole, lead_part, turns, shifted, coarse, rest, fine = (
+def turns_per_position(nc, pool, lam):
+    names = ("lead", "last", "whole", "small", "lead_part", "turns", "shifted", "coarse", "rest", "fine")
+    lead, last, whole, small, lead_part, turns, shifted, coarse, rest, fine = (
         pool.tile([P, PLANES], F32, name=name) for name in names
     )
-    nc.vector.tensor_copy(out=lam[:], in_=lam_bf[:].rearrange("p g t -> p (g t)"))
-    nc.vector.tensor_scalar(out=lead[:], in0=lam[:], scalar1=INV_2PI_A, scalar2=None, op0=ALU.mult)
+    nc.vector.tensor_scalar(out=lead[:], in0=lam, scalar1=INV_2PI_A, scalar2=None, op0=ALU.mult)
+    nc.vector.tensor_scalar(out=last[:], in0=lam, scalar1=INV_2PI_C, scalar2=None, op0=ALU.mult)
     nc.vector.tensor_scalar(
         out=whole[:], in0=lead[:], scalar1=ROUND, scalar2=ROUND, op0=ALU.add, op1=ALU.subtract
     )
-    nc.vector.tensor_tensor(out=lead_part[:], in0=lead[:], in1=whole[:], op=ALU.subtract)
     nc.vector.scalar_tensor_tensor(
-        out=turns[:], in0=lam[:], scalar=INV_2PI_B, in1=lead_part[:], op0=ALU.mult, op1=ALU.add
+        out=small[:], in0=lam, scalar=INV_2PI_B, in1=last[:], op0=ALU.mult, op1=ALU.add
     )
+    nc.vector.tensor_tensor(out=lead_part[:], in0=lead[:], in1=whole[:], op=ALU.subtract)
+    nc.vector.tensor_tensor(out=turns[:], in0=lead_part[:], in1=small[:], op=ALU.add)
     nc.vector.tensor_scalar(
         out=shifted[:], in0=turns[:], scalar1=GRID, scalar2=ROUND, op0=ALU.mult, op1=ALU.add
     )
@@ -59,12 +61,7 @@ def turns_per_position(nc, pool, lam_bf):
         out=coarse[:], in0=shifted[:], scalar1=ROUND, scalar2=1.0 / GRID, op0=ALU.subtract, op1=ALU.mult
     )
     nc.vector.tensor_tensor(out=rest[:], in0=lead_part[:], in1=coarse[:], op=ALU.subtract)
-    nc.vector.scalar_tensor_tensor(
-        out=rest[:], in0=lam[:], scalar=INV_2PI_B, in1=rest[:], op0=ALU.mult, op1=ALU.add
-    )
-    nc.vector.scalar_tensor_tensor(
-        out=fine[:], in0=lam[:], scalar=INV_2PI_C, in1=rest[:], op0=ALU.mult, op1=ALU.add
-    )
+    nc.vector.tensor_tensor(out=fine[:], in0=rest[:], in1=small[:], op=ALU.add)
     return coarse, fine
 
 
@@ -85,8 +82,8 @@ def tile_dlrkernel_e_kernel(tc, W_words, W_scales, Lambda_im, L, out):
         stream = stack.enter_context(tc.tile_pool(name="stream", bufs=4))
         banks = stack.enter_context(tc.psum_pool(name="banks", bufs=1))
 
-        lam_bf = keep.tile([P, GROUPS, PACK], BF16)
-        nc.sync.dma_start(out=lam_bf[:], in_=Lambda_im.rearrange("(g p t) -> p g t", p=P, t=PACK))
+        lam = keep.tile([P, GROUPS, PACK], BF16)
+        nc.sync.dma_start(out=lam[:], in_=Lambda_im.rearrange("(g p t) -> p g t", p=P, t=PACK))
         w_scales = keep.tile([P, GROUPS, H], U8, align_bytes=64)
         nc.vector.memset(w_scales[:].rearrange("p g h -> p (g h)").bitcast(I32), 0)
         for quadrant in range(4):
@@ -99,23 +96,23 @@ def tile_dlrkernel_e_kernel(tc, W_words, W_scales, Lambda_im, L, out):
             out=w_words[:].bitcast(I32), in_=W_words.rearrange("g p h t -> p g (h t)").bitcast(I32)
         )
 
-        args = keep.tile([P, ARGS], F32)
-        for k, step in enumerate(STEPS):
-            nc.vector.memset(args[:, k : k + 1], float(step))
-        seed_positions = keep.tile([P, SEED], I32)
-        nc.gpsimd.iota(seed_positions[:], pattern=[[1, SEED]], base=CENTRE - SEED // 2, channel_multiplier=0)
-        nc.vector.tensor_copy(out=args[:, len(STEPS) :], in_=seed_positions[:])
-
-        coarse, fine = turns_per_position(nc, keep, lam_bf)
-
-        lower = [keep.tile([P, PACK, HALF], F32, name="lower%d" % g) for g in range(GROUPS)]
+        lower = keep.tile([P, PLANES, PLANE], F32)
         twice_cos = keep.tile([P, PLANES, len(STEPS)], F32)
 
-        with tc.tile_pool(name="seed_work", bufs=1) as work:
+        with tc.tile_pool(name="start", bufs=1) as start:
+            args = start.tile([P, ARGS], F32)
+            for k, step in enumerate(STEPS):
+                nc.vector.memset(args[:, k : k + 1], float(step))
+            seed_positions = start.tile([P, SEED + 1], I32)
+            nc.gpsimd.iota(seed_positions[:], pattern=[[1, SEED + 1]], base=0, channel_multiplier=0)
+            nc.vector.tensor_copy(out=args[:, len(STEPS) :], in_=seed_positions[:])
+
+            coarse, fine = turns_per_position(nc, start, lam[:].rearrange("p g t -> p (g t)"))
+
             shape = [P, PLANES, ARGS]
             args_of_all = args[:].unsqueeze(1).to_broadcast(shape)
-            turn = work.tile(shape, F32)
-            other = work.tile(shape, F32)
+            turn = start.tile(shape, F32)
+            other = start.tile(shape, F32)
             nc.vector.tensor_tensor(
                 out=turn[:], in0=args_of_all, in1=coarse[:].unsqueeze(2).to_broadcast(shape), op=ALU.mult
             )
@@ -130,64 +127,71 @@ def tile_dlrkernel_e_kernel(tc, W_words, W_scales, Lambda_im, L, out):
             nc.vector.scalar_tensor_tensor(
                 out=other[:], in0=turn[:], scalar=-1.0, in1=turn[:], op0=ALU.mult, op1=ALU.max
             )
-            cos_step = work.tile([P, PLANES, len(STEPS)], F32)
+            cos_step = start.tile([P, PLANES, len(STEPS)], F32)
             nc.scalar.activation(
-                out=cos_step[:],
-                in_=other[:, :, : len(STEPS)],
-                func=mybir.ActivationFunctionType.Sin,
+                out=cos_step[:], in_=other[:, :, : len(STEPS)], func=SIN, bias=math.pi / 2, scale=-2.0 * math.pi
+            )
+            nc.scalar.activation(
+                out=lower[:, :, : SEED + 1],
+                in_=other[:, :, len(STEPS) :],
+                func=SIN,
                 bias=math.pi / 2,
                 scale=-2.0 * math.pi,
             )
             nc.vector.tensor_scalar(out=twice_cos[:], in0=cos_step[:], scalar1=2.0, scalar2=None, op0=ALU.mult)
-            for g in range(GROUPS):
-                nc.scalar.activation(
-                    out=lower[g][:, :, CENTRE - SEED // 2 : CENTRE + SEED // 2],
-                    in_=other[:, PACK * g : PACK * (g + 1), len(STEPS) :],
-                    func=mybir.ActivationFunctionType.Sin,
-                    bias=math.pi / 2,
-                    scale=-2.0 * math.pi,
+
+            for k in range(SHORT_STEPS):
+                step = STEPS[k]
+                product = start.tile([P, PLANES, step], F32, name="product%d" % k)
+                nc.vector.tensor_tensor(
+                    out=product[:],
+                    in0=lower[:, :, 1 : step + 1],
+                    in1=twice_cos[:, :, k : k + 1].to_broadcast([P, PLANES, step]),
+                    op=ALU.mult,
+                )
+                nc.vector.tensor_tensor(
+                    out=lower[:, :, step + 1 : 2 * step + 1],
+                    in0=product[:],
+                    in1=lower[:, :, step - 1 :: -1],
+                    op=ALU.subtract,
                 )
 
         upper = stack.enter_context(tc.tile_pool(name="upper", bufs=2))
 
-        def next_columns(out_columns, middle, scale, far):
-            nc.vector.scalar_tensor_tensor(
-                out=out_columns, in0=middle, scalar=scale, in1=far, op0=ALU.mult, op1=ALU.subtract
-            )
-
         def grow_lower_half(g):
-            for k, step in enumerate(LOWER_STEPS):
-                for t in range(PACK):
-                    blocks = lower[g][:, t, CENTRE - 2 * step : CENTRE + 2 * step].rearrange(
-                        "p (b j) -> p b j", b=4
-                    )
-                    next_columns(
-                        blocks[:, 0:4:3, :],
-                        blocks[:, 1:3, :],
-                        twice_cos[:, PACK * g + t, k : k + 1],
-                        blocks[:, 2:0:-1, :],
+            for k in range(SHORT_STEPS, LOWER_STEPS):
+                step = STEPS[k]
+                for q in range(PACK * g, PACK * (g + 1)):
+                    nc.vector.scalar_tensor_tensor(
+                        out=lower[:, q, step + 1 : 2 * step + 1],
+                        in0=lower[:, q, 1 : step + 1],
+                        scalar=twice_cos[:, q, k : k + 1],
+                        in1=lower[:, q, step - 1 :: -1],
+                        op0=ALU.mult,
+                        op1=ALU.subtract,
                     )
 
         def odd_upper_columns(g):
-            odd = [upper.tile([P, PACK, CHUNK // 2], F32, name="odd%d" % c) for c in range(CHUNKS)]
-            for c in range(CHUNKS):
-                for t in range(PACK):
-                    scale = twice_cos[:, PACK * g + t, len(LOWER_STEPS) : len(STEPS)]
-                    low_odd = lower[g][:, t, 1:CENTRE:2]
-                    high_odd = lower[g][:, t, CENTRE + 1 : HALF : 2]
-                    if c == 0:
-                        next_columns(odd[0][:, t, :], high_odd, scale, low_odd)
-                    else:
-                        next_columns(odd[1][:, t, :], odd[0][:, t, :], scale, high_odd)
+            odd = upper.tile([P, PACK, HALF // 2], F32)
+            for t in range(PACK):
+                q = PACK * g + t
+                nc.vector.scalar_tensor_tensor(
+                    out=odd[:, t, :],
+                    in0=lower[:, q, 1:HALF:2],
+                    scalar=twice_cos[:, q, LOWER_STEPS : LOWER_STEPS + 1],
+                    in1=lower[:, q, HALF - 1 : 0 : -2],
+                    op0=ALU.mult,
+                    op1=ALU.subtract,
+                )
             return odd
 
         def squares_for_even_upper_columns(g):
             square = [upper.tile([P, PACK * CHUNK // 2], F32, name="square%d" % c) for c in range(CHUNKS)]
             for c in range(CHUNKS):
-                first = CENTRE + c * CHUNK // 2
+                first = (HALF + c * CHUNK) // 2
                 nc.scalar.square(
                     out=by_runs_interleaved(square[c][:]),
-                    in_=by_runs_of_planes(lower[g][:, :, first : first + CHUNK // 2]),
+                    in_=by_runs_of_planes(lower[:, PACK * g : PACK * (g + 1), first : first + CHUNK // 2]),
                 )
             return square
 
@@ -231,7 +235,7 @@ def tile_dlrkernel_e_kernel(tc, W_words, W_scales, Lambda_im, L, out):
             for c in range(CHUNKS):
                 nc.scalar.copy(
                     out=by_runs_interleaved(grouped[c][:]),
-                    in_=by_runs_of_planes(lower[g][:, :, CHUNK * c : CHUNK * (c + 1)]),
+                    in_=by_runs_of_planes(lower[:, PACK * g : PACK * (g + 1), CHUNK * c : CHUNK * (c + 1)]),
                 )
             if g + 1 < GROUPS:
                 grow_lower_half(g + 1)
@@ -245,7 +249,8 @@ def tile_dlrkernel_e_kernel(tc, W_words, W_scales, Lambda_im, L, out):
             grouped = [stream.tile([P, PACK * CHUNK], BF16, name="grouped", align_bytes=64) for c in range(CHUNKS)]
             for c in range(CHUNKS):
                 nc.scalar.copy(
-                    out=by_runs_interleaved(grouped[c][:, PACK * CHUNK // 2 :]), in_=by_runs_of_planes(odd[c][:])
+                    out=by_runs_interleaved(grouped[c][:, PACK * CHUNK // 2 :]),
+                    in_=by_runs_of_planes(odd[:, :, c * CHUNK // 2 : (c + 1) * CHUNK // 2]),
                 )
             this_square = square
             if g + 1 < GROUPS:

@@ -26,43 +26,15 @@ CHUNK = 512
 CHUNKS = HALF // CHUNK
 RUN = 4
 PLANE = HALF + RUN
-SEED = 16
-STEPS = (16, 32, 64, 128, 256, 512, 1024)
-SHORT_STEPS = 2
+SEED = 8
+STEPS = (8, 16, 32, 64, 128, 256, 512, 1024)
+SHORT_STEPS = 3
 LOWER_STEPS = len(STEPS) - 1
-ARGS = len(STEPS) + SEED + 1
+ARGS = SEED + len(STEPS) - 1
+PARTS = ((0, 8), (8, 32))
 
-ROUND = 12582912.0
-INV_2PI_A = 41722.0 * 2.0**-18
-INV_2PI_B = -63779.0 * 2.0**-35
-INV_2PI_C = -13037483.0 * 2.0**-60
-GRID = 4096.0
-
-
-def turns_per_position(nc, pool, lam):
-    names = ("lead", "last", "whole", "small", "lead_part", "turns", "shifted", "coarse", "rest", "fine")
-    lead, last, whole, small, lead_part, turns, shifted, coarse, rest, fine = (
-        pool.tile([P, PLANES], F32, name=name) for name in names
-    )
-    nc.vector.tensor_scalar(out=lead[:], in0=lam, scalar1=INV_2PI_A, scalar2=None, op0=ALU.mult)
-    nc.vector.tensor_scalar(out=last[:], in0=lam, scalar1=INV_2PI_C, scalar2=None, op0=ALU.mult)
-    nc.vector.tensor_scalar(
-        out=whole[:], in0=lead[:], scalar1=ROUND, scalar2=ROUND, op0=ALU.add, op1=ALU.subtract
-    )
-    nc.vector.scalar_tensor_tensor(
-        out=small[:], in0=lam, scalar=INV_2PI_B, in1=last[:], op0=ALU.mult, op1=ALU.add
-    )
-    nc.vector.tensor_tensor(out=lead_part[:], in0=lead[:], in1=whole[:], op=ALU.subtract)
-    nc.vector.tensor_tensor(out=turns[:], in0=lead_part[:], in1=small[:], op=ALU.add)
-    nc.vector.tensor_scalar(
-        out=shifted[:], in0=turns[:], scalar1=GRID, scalar2=ROUND, op0=ALU.mult, op1=ALU.add
-    )
-    nc.vector.tensor_scalar(
-        out=coarse[:], in0=shifted[:], scalar1=ROUND, scalar2=1.0 / GRID, op0=ALU.subtract, op1=ALU.mult
-    )
-    nc.vector.tensor_tensor(out=rest[:], in0=lead_part[:], in1=coarse[:], op=ALU.subtract)
-    nc.vector.tensor_tensor(out=fine[:], in0=rest[:], in1=small[:], op=ALU.add)
-    return coarse, fine
+TWO_PI_HEAD = 6434.0 / 1024.0
+TWO_PI_TAIL = 2.0 * math.pi - TWO_PI_HEAD
 
 
 def by_runs_of_planes(planes):
@@ -99,62 +71,75 @@ def tile_dlrkernel_e_kernel(tc, W_words, W_scales, Lambda_im, L, out):
         lower = keep.tile([P, PLANES, PLANE], F32)
         twice_cos = keep.tile([P, PLANES, len(STEPS)], F32)
 
-        with tc.tile_pool(name="start", bufs=1) as start:
-            args = start.tile([P, ARGS], F32)
-            for k, step in enumerate(STEPS):
-                nc.vector.memset(args[:, k : k + 1], float(step))
-            seed_positions = start.tile([P, SEED + 1], I32)
-            nc.gpsimd.iota(seed_positions[:], pattern=[[1, SEED + 1]], base=0, channel_multiplier=0)
-            nc.vector.tensor_copy(out=args[:, len(STEPS) :], in_=seed_positions[:])
+        start = stack.enter_context(tc.tile_pool(name="start", bufs=1))
+        nc.vector.memset(lower[:, :, 0:1], 1.0)
+        args = start.tile([P, ARGS], F32)
+        for k, step in enumerate(STEPS[1:]):
+            nc.vector.memset(args[:, SEED + k : SEED + k + 1], float(step))
+        seed_positions = start.tile([P, SEED], I32)
+        nc.gpsimd.iota(seed_positions[:], pattern=[[1, SEED]], base=1, channel_multiplier=0)
+        nc.vector.tensor_copy(out=args[:, :SEED], in_=seed_positions[:])
+        lam_by_plane = lam[:].rearrange("p g t -> p (g t)")
 
-            coarse, fine = turns_per_position(nc, start, lam[:].rearrange("p g t -> p (g t)"))
-
-            shape = [P, PLANES, ARGS]
-            args_of_all = args[:].unsqueeze(1).to_broadcast(shape)
-            turn = start.tile(shape, F32)
-            other = start.tile(shape, F32)
+        def seed_angles(part):
+            first, end = part
+            shape = [P, end - first, ARGS]
+            angle = start.tile(shape, F32, name="angle%d" % first)
+            periods = start.tile(shape, I32, name="periods%d" % first)
             nc.vector.tensor_tensor(
-                out=turn[:], in0=args_of_all, in1=coarse[:].unsqueeze(2).to_broadcast(shape), op=ALU.mult
+                out=angle[:],
+                in0=args[:].unsqueeze(1).to_broadcast(shape),
+                in1=lam_by_plane[:, first:end].unsqueeze(2).to_broadcast(shape),
+                op=ALU.mult,
             )
             nc.vector.tensor_scalar(
-                out=other[:], in0=turn[:], scalar1=ROUND, scalar2=ROUND, op0=ALU.add, op1=ALU.subtract
+                out=periods[:], in0=angle[:], scalar1=0.5 / math.pi, scalar2=None, op0=ALU.mult
             )
-            nc.vector.tensor_tensor(out=turn[:], in0=turn[:], in1=other[:], op=ALU.subtract)
-            nc.vector.tensor_tensor(
-                out=other[:], in0=args_of_all, in1=fine[:].unsqueeze(2).to_broadcast(shape), op=ALU.mult
-            )
-            nc.vector.tensor_tensor(out=turn[:], in0=turn[:], in1=other[:], op=ALU.add)
             nc.vector.scalar_tensor_tensor(
-                out=other[:], in0=turn[:], scalar=-1.0, in1=turn[:], op0=ALU.mult, op1=ALU.max
+                out=angle[:], in0=periods[:], scalar=-TWO_PI_HEAD, in1=angle[:], op0=ALU.mult, op1=ALU.add
             )
-            cos_step = start.tile([P, PLANES, len(STEPS)], F32)
-            nc.scalar.activation(
-                out=cos_step[:], in_=other[:, :, : len(STEPS)], func=SIN, bias=math.pi / 2, scale=-2.0 * math.pi
+            nc.vector.scalar_tensor_tensor(
+                out=angle[:], in0=periods[:], scalar=-TWO_PI_TAIL, in1=angle[:], op0=ALU.mult, op1=ALU.add
             )
-            nc.scalar.activation(
-                out=lower[:, :, : SEED + 1],
-                in_=other[:, :, len(STEPS) :],
-                func=SIN,
-                bias=math.pi / 2,
-                scale=-2.0 * math.pi,
-            )
-            nc.vector.tensor_scalar(out=twice_cos[:], in0=cos_step[:], scalar1=2.0, scalar2=None, op0=ALU.mult)
+            return angle
 
+        cos_step = start.tile([P, PLANES, len(STEPS)], F32)
+
+        def seed_cosines(part, angle):
+            first, end = part
+            nc.scalar.activation(out=angle[:], in_=angle[:], func=mybir.ActivationFunctionType.Abs)
+            nc.scalar.activation(
+                out=cos_step[:, first:end, :], in_=angle[:, :, SEED - 1 :], func=SIN, bias=math.pi / 2, scale=-1.0
+            )
+            nc.scalar.activation(
+                out=lower[:, first:end, 1 : SEED + 1], in_=angle[:, :, :SEED], func=SIN, bias=math.pi / 2, scale=-1.0
+            )
+
+        def take_short_steps(part):
+            first, end = part
+            nc.vector.tensor_scalar(
+                out=twice_cos[:, first:end, :], in0=cos_step[:, first:end, :], scalar1=2.0, scalar2=None, op0=ALU.mult
+            )
             for k in range(SHORT_STEPS):
                 step = STEPS[k]
-                product = start.tile([P, PLANES, step], F32, name="product%d" % k)
+                shape = [P, end - first, step]
+                product = start.tile(shape, F32, name="product%d_%d" % (first, k))
                 nc.vector.tensor_tensor(
                     out=product[:],
-                    in0=lower[:, :, 1 : step + 1],
-                    in1=twice_cos[:, :, k : k + 1].to_broadcast([P, PLANES, step]),
+                    in0=lower[:, first:end, 1 : step + 1],
+                    in1=twice_cos[:, first:end, k : k + 1].to_broadcast(shape),
                     op=ALU.mult,
                 )
                 nc.vector.tensor_tensor(
-                    out=lower[:, :, step + 1 : 2 * step + 1],
+                    out=lower[:, first:end, step + 1 : 2 * step + 1],
                     in0=product[:],
-                    in1=lower[:, :, step - 1 :: -1],
+                    in1=lower[:, first:end, step - 1 :: -1],
                     op=ALU.subtract,
                 )
+
+        angles = [seed_angles(part) for part in PARTS]
+        for part, angle in zip(PARTS, angles):
+            seed_cosines(part, angle)
 
         upper = stack.enter_context(tc.tile_pool(name="upper", bufs=2))
 
@@ -216,20 +201,24 @@ def tile_dlrkernel_e_kernel(tc, W_words, W_scales, Lambda_im, L, out):
                 for c in range(CHUNKS)
             ]
 
+        def store_bank(column, bank, h, strands, copy):
+            result = stream.tile([P, CHUNK], F32, name="result", bufs=CHUNKS * H_TILES)
+            copy(
+                out=result[:].rearrange("p (r e) -> p r e", e=strands),
+                in_=bank[:].rearrange("p (e r) -> p r e", e=strands),
+            )
+            nc.sync.dma_start(out=out[0, P * h : P * (h + 1), column : column + CHUNK], in_=result[:])
+
         def store_half(first_column, sums, strands):
             for c in range(CHUNKS):
                 for h in range(H_TILES):
-                    result = stream.tile([P, CHUNK], F32, name="result", bufs=CHUNKS * H_TILES)
                     copy = nc.scalar.copy if (c + h) % 2 == 0 else nc.vector.tensor_copy
-                    copy(
-                        out=result[:].rearrange("p (r e) -> p r e", e=strands),
-                        in_=sums[c][h][:].rearrange("p (e r) -> p r e", e=strands),
-                    )
-                    columns = first_column + CHUNK * c
-                    nc.sync.dma_start(out=out[0, P * h : P * (h + 1), columns : columns + CHUNK], in_=result[:])
+                    store_bank(first_column + CHUNK * c, sums[c][h], h, strands, copy)
 
         sums = open_banks()
+        take_short_steps(PARTS[0])
         grow_lower_half(0)
+        take_short_steps(PARTS[1])
         for g in range(GROUPS):
             grouped = [stream.tile([P, PACK * CHUNK], BF16, name="grouped", align_bytes=64) for c in range(CHUNKS)]
             for c in range(CHUNKS):
@@ -245,29 +234,60 @@ def tile_dlrkernel_e_kernel(tc, W_words, W_scales, Lambda_im, L, out):
             for c in range(CHUNKS):
                 quantise_and_multiply(g, grouped[c], sums[c])
 
-        for g in range(GROUPS):
-            grouped = [stream.tile([P, PACK * CHUNK], BF16, name="grouped", align_bytes=64) for c in range(CHUNKS)]
+        def new_grouped():
+            return [stream.tile([P, PACK * CHUNK], BF16, name="grouped", align_bytes=64) for c in range(CHUNKS)]
+
+        def interleave_odd(grouped, odd, c):
+            nc.scalar.copy(
+                out=by_runs_interleaved(grouped[c][:, PACK * CHUNK // 2 :]),
+                in_=by_runs_of_planes(odd[:, :, c * CHUNK // 2 : (c + 1) * CHUNK // 2]),
+            )
+
+        def finish_even(grouped, square, c):
+            nc.vector.tensor_scalar(
+                out=grouped[c][:, : PACK * CHUNK // 2],
+                in0=square[c][:],
+                scalar1=2.0,
+                scalar2=1.0,
+                op0=ALU.mult,
+                op1=ALU.subtract,
+            )
+
+        for g in range(GROUPS - 2):
+            grouped = new_grouped()
             for c in range(CHUNKS):
-                nc.scalar.copy(
-                    out=by_runs_interleaved(grouped[c][:, PACK * CHUNK // 2 :]),
-                    in_=by_runs_of_planes(odd[:, :, c * CHUNK // 2 : (c + 1) * CHUNK // 2]),
-                )
+                interleave_odd(grouped, odd, c)
             this_square = square
-            if g + 1 < GROUPS:
-                square = squares_for_even_upper_columns(g + 1)
-                odd = odd_upper_columns(g + 1)
+            square = squares_for_even_upper_columns(g + 1)
+            odd = odd_upper_columns(g + 1)
             for c in range(CHUNKS):
-                nc.vector.tensor_scalar(
-                    out=grouped[c][:, : PACK * CHUNK // 2],
-                    in0=this_square[c][:],
-                    scalar1=2.0,
-                    scalar2=1.0,
-                    op0=ALU.mult,
-                    op1=ALU.subtract,
-                )
+                finish_even(grouped, this_square, c)
             if g == 0:
                 store_half(0, sums, 1)
                 sums = open_banks()
             for c in range(CHUNKS):
                 quantise_and_multiply(g, grouped[c], sums[c])
-        store_half(HALF, sums, 2)
+
+        last = (GROUPS - 2, GROUPS - 1)
+        grouped = {g: new_grouped() for g in last}
+        squares = {last[0]: square}
+        odds = {last[0]: odd}
+        interleave_odd(grouped[last[0]], odds[last[0]], 0)
+        squares[last[1]] = squares_for_even_upper_columns(last[1])
+        odds[last[1]] = odd_upper_columns(last[1])
+        interleave_odd(grouped[last[1]], odds[last[1]], 0)
+        interleave_odd(grouped[last[0]], odds[last[0]], 1)
+        interleave_odd(grouped[last[1]], odds[last[1]], 1)
+        for g in last:
+            finish_even(grouped[g], squares[g], 0)
+        for g in last:
+            quantise_and_multiply(g, grouped[g][0], sums[0])
+        finish_even(grouped[last[0]], squares[last[0]], 1)
+        finish_even(grouped[last[1]], squares[last[1]], 1)
+        quantise_and_multiply(last[0], grouped[last[0]][1], sums[1])
+        for h in range(H_TILES):
+            store_bank(HALF, sums[0][h], h, 2, nc.scalar.copy)
+        quantise_and_multiply(last[1], grouped[last[1]][1], sums[1])
+        for h in range(H_TILES):
+            copy = nc.scalar.copy if h % 2 == 0 else nc.vector.tensor_copy
+            store_bank(HALF + CHUNK, sums[1][h], h, 2, copy)

@@ -157,7 +157,7 @@ def tile_dlrkernel_e_kernel(tc, W_words, W_scales, Lambda_im, L, out):
                     )
 
         def odd_upper_columns(g):
-            odd = upper.tile([P, PACK, HALF // 2], F32)
+            odd = upper.tile([P, PACK, HALF // 2], BF16)
             for t in range(PACK):
                 q = PACK * g + t
                 nc.vector.scalar_tensor_tensor(

@@ -24,8 +24,8 @@ COLUMNS = 2048
 HALF = COLUMNS // 2
 CHUNK = 512
 CHUNKS = HALF // CHUNK
-RUN = 4
-PLANE = HALF + RUN
+RUN = 2
+PLANE = HALF + 4
 SEED = 8
 STEPS = (8, 16, 32, 64, 128, 256, 512, 1024)
 SHORT_STEPS = 3

@@ -29,9 +29,11 @@ PLANE = HALF + 4
 SEED = 8
 STEPS = (8, 16, 32, 64, 128, 256, 512, 1024)
 SHORT_STEPS = 3
+RESULTS = 8
+EARLY_SQUARES = {1: (0, 0), 2: (0, 1), 3: (1, 0), 4: (1, 1)}
 LOWER_STEPS = len(STEPS) - 1
 ARGS = SEED + len(STEPS) - 1
-PARTS = ((0, 8), (8, 32))
+PARTS = ((0, PLANES // 2), (PLANES // 2, PLANES))
 
 TWO_PI_HEAD = 6434.0 / 1024.0
 TWO_PI_TAIL = 2.0 * math.pi - TWO_PI_HEAD
@@ -51,7 +53,7 @@ def tile_dlrkernel_e_kernel(tc, W_words, W_scales, Lambda_im, L, out):
     with ExitStack() as stack:
         stack.enter_context(tc.manual_schedule())
         keep = stack.enter_context(tc.tile_pool(name="keep", bufs=1))
-        stream = stack.enter_context(tc.tile_pool(name="stream", bufs=4))
+        stream = stack.enter_context(tc.tile_pool(name="stream", bufs=2))
         banks = stack.enter_context(tc.psum_pool(name="banks", bufs=1))
 
         lam = keep.tile([P, GROUPS, PACK], BF16)
@@ -71,75 +73,76 @@ def tile_dlrkernel_e_kernel(tc, W_words, W_scales, Lambda_im, L, out):
         lower = keep.tile([P, PLANES, PLANE], F32)
         twice_cos = keep.tile([P, PLANES, len(STEPS)], F32)
 
-        start = stack.enter_context(tc.tile_pool(name="start", bufs=1))
-        nc.vector.memset(lower[:, :, 0:1], 1.0)
-        args = start.tile([P, ARGS], F32)
-        for k, step in enumerate(STEPS[1:]):
-            nc.vector.memset(args[:, SEED + k : SEED + k + 1], float(step))
-        seed_positions = start.tile([P, SEED], I32)
-        nc.gpsimd.iota(seed_positions[:], pattern=[[1, SEED]], base=1, channel_multiplier=0)
-        nc.vector.tensor_copy(out=args[:, :SEED], in_=seed_positions[:])
-        lam_by_plane = lam[:].rearrange("p g t -> p (g t)")
+        with tc.tile_pool(name="start", bufs=1) as start:
+            nc.vector.memset(lower[:, :, 0:1], 1.0)
+            args = start.tile([P, ARGS], F32)
+            for k, step in enumerate(STEPS[1:]):
+                nc.vector.memset(args[:, SEED + k : SEED + k + 1], float(step))
+            seed_positions = start.tile([P, SEED], I32)
+            nc.gpsimd.iota(seed_positions[:], pattern=[[1, SEED]], base=1, channel_multiplier=0)
+            nc.vector.tensor_copy(out=args[:, :SEED], in_=seed_positions[:])
+            unused = start.tile([P, 1], F32)
+            nc.scalar.activation(out=unused[:], in_=lower[:, 0, 0:1], func=SIN)
+            lam_by_plane = lam[:].rearrange("p g t -> p (g t)")
 
-        def seed_angles(part):
-            first, end = part
-            shape = [P, end - first, ARGS]
-            angle = start.tile(shape, F32, name="angle%d" % first)
-            periods = start.tile(shape, I32, name="periods%d" % first)
-            nc.vector.tensor_tensor(
-                out=angle[:],
-                in0=args[:].unsqueeze(1).to_broadcast(shape),
-                in1=lam_by_plane[:, first:end].unsqueeze(2).to_broadcast(shape),
-                op=ALU.mult,
-            )
-            nc.vector.tensor_scalar(
-                out=periods[:], in0=angle[:], scalar1=0.5 / math.pi, scalar2=None, op0=ALU.mult
-            )
-            nc.vector.scalar_tensor_tensor(
-                out=angle[:], in0=periods[:], scalar=-TWO_PI_HEAD, in1=angle[:], op0=ALU.mult, op1=ALU.add
-            )
-            nc.vector.scalar_tensor_tensor(
-                out=angle[:], in0=periods[:], scalar=-TWO_PI_TAIL, in1=angle[:], op0=ALU.mult, op1=ALU.add
-            )
-            return angle
-
-        cos_step = start.tile([P, PLANES, len(STEPS)], F32)
-
-        def seed_cosines(part, angle):
-            first, end = part
-            nc.scalar.activation(out=angle[:], in_=angle[:], func=mybir.ActivationFunctionType.Abs)
-            nc.scalar.activation(
-                out=cos_step[:, first:end, :], in_=angle[:, :, SEED - 1 :], func=SIN, bias=math.pi / 2, scale=-1.0
-            )
-            nc.scalar.activation(
-                out=lower[:, first:end, 1 : SEED + 1], in_=angle[:, :, :SEED], func=SIN, bias=math.pi / 2, scale=-1.0
-            )
-
-        def take_short_steps(part):
-            first, end = part
-            nc.vector.tensor_scalar(
-                out=twice_cos[:, first:end, :], in0=cos_step[:, first:end, :], scalar1=2.0, scalar2=None, op0=ALU.mult
-            )
-            for k in range(SHORT_STEPS):
-                step = STEPS[k]
-                shape = [P, end - first, step]
-                product = start.tile(shape, F32, name="product%d_%d" % (first, k))
+            shapes = [[P, end - first, ARGS] for first, end in PARTS]
+            angles = [start.tile(shape, F32, name="angle%d" % i) for i, shape in enumerate(shapes)]
+            periods = [start.tile(shape, I32, name="periods%d" % i) for i, shape in enumerate(shapes)]
+            cos_step = start.tile([P, PLANES, len(STEPS)], F32)
+            for (first, end), shape, angle in zip(PARTS, shapes, angles):
                 nc.vector.tensor_tensor(
-                    out=product[:],
-                    in0=lower[:, first:end, 1 : step + 1],
-                    in1=twice_cos[:, first:end, k : k + 1].to_broadcast(shape),
+                    out=angle[:],
+                    in0=args[:].unsqueeze(1).to_broadcast(shape),
+                    in1=lam_by_plane[:, first:end].unsqueeze(2).to_broadcast(shape),
                     op=ALU.mult,
                 )
-                nc.vector.tensor_tensor(
-                    out=lower[:, first:end, step + 1 : 2 * step + 1],
-                    in0=product[:],
-                    in1=lower[:, first:end, step - 1 :: -1],
-                    op=ALU.subtract,
+            for angle, period in zip(angles, periods):
+                nc.vector.tensor_scalar(
+                    out=period[:], in0=angle[:], scalar1=0.5 / math.pi, scalar2=None, op0=ALU.mult
                 )
-
-        angles = [seed_angles(part) for part in PARTS]
-        for part, angle in zip(PARTS, angles):
-            seed_cosines(part, angle)
+            for share in (TWO_PI_HEAD, TWO_PI_TAIL):
+                for angle, period in zip(angles, periods):
+                    nc.vector.scalar_tensor_tensor(
+                        out=angle[:], in0=period[:], scalar=-share, in1=angle[:], op0=ALU.mult, op1=ALU.add
+                    )
+            for (first, end), angle in zip(PARTS, angles):
+                nc.scalar.activation(out=angle[:], in_=angle[:], func=mybir.ActivationFunctionType.Abs)
+                nc.scalar.activation(
+                    out=cos_step[:, first:end, :], in_=angle[:, :, SEED - 1 :], func=SIN, bias=math.pi / 2, scale=-1.0
+                )
+                nc.scalar.activation(
+                    out=lower[:, first:end, 1 : SEED + 1],
+                    in_=angle[:, :, :SEED],
+                    func=SIN,
+                    bias=math.pi / 2,
+                    scale=-1.0,
+                )
+            for first, end in PARTS:
+                nc.vector.tensor_scalar(
+                    out=twice_cos[:, first:end, :],
+                    in0=cos_step[:, first:end, :],
+                    scalar1=2.0,
+                    scalar2=None,
+                    op0=ALU.mult,
+                )
+            for k in range(SHORT_STEPS):
+                step = STEPS[k]
+                shapes = [[P, end - first, step] for first, end in PARTS]
+                products = [start.tile(shape, F32, name="product%d_%d" % (i, k)) for i, shape in enumerate(shapes)]
+                for (first, end), shape, product in zip(PARTS, shapes, products):
+                    nc.vector.tensor_tensor(
+                        out=product[:],
+                        in0=lower[:, first:end, 1 : step + 1],
+                        in1=twice_cos[:, first:end, k : k + 1].to_broadcast(shape),
+                        op=ALU.mult,
+                    )
+                for (first, end), product in zip(PARTS, products):
+                    nc.vector.tensor_tensor(
+                        out=lower[:, first:end, step + 1 : 2 * step + 1],
+                        in0=product[:],
+                        in1=lower[:, first:end, step - 1 :: -1],
+                        op=ALU.subtract,
+                    )
 
         upper = stack.enter_context(tc.tile_pool(name="upper", bufs=2))
 
@@ -157,7 +160,7 @@ def tile_dlrkernel_e_kernel(tc, W_words, W_scales, Lambda_im, L, out):
                     )
 
         def odd_upper_columns(g):
-            odd = upper.tile([P, PACK, HALF // 2], BF16)
+            odd = upper.tile([P, PACK, HALF // 2], BF16, bufs=3)
             for t in range(PACK):
                 q = PACK * g + t
                 nc.vector.scalar_tensor_tensor(
@@ -170,27 +173,58 @@ def tile_dlrkernel_e_kernel(tc, W_words, W_scales, Lambda_im, L, out):
                 )
             return odd
 
-        def squares_for_even_upper_columns(g):
-            square = [upper.tile([P, PACK * CHUNK // 2], F32, name="square%d" % c) for c in range(CHUNKS)]
-            for c in range(CHUNKS):
-                first = (HALF + c * CHUNK) // 2
-                nc.scalar.square(
-                    out=by_runs_interleaved(square[c][:]),
-                    in_=by_runs_of_planes(lower[:, PACK * g : PACK * (g + 1), first : first + CHUNK // 2]),
-                )
-            return square
+        def new_squares():
+            return upper.tile([P, PACK * HALF // 2], F32, name="square")
 
-        def quantise_and_multiply(g, grouped, sums):
-            codes = stream.tile([P, CHUNK], U32, align_bytes=64)
-            scales = stream.tile([P, CHUNK], U8, align_bytes=64)
-            nc.vector.quantize_mx(out=codes[:].bitcast(FP8X4), scales=scales[:], in_=grouped[:])
+        def make_squares(square, g, c):
+            width = PACK * CHUNK // 2
+            first = (HALF + c * CHUNK) // 2
+            nc.scalar.square(
+                out=by_runs_interleaved(square[:, c * width : (c + 1) * width]),
+                in_=by_runs_of_planes(lower[:, PACK * g : PACK * (g + 1), first : first + CHUNK // 2]),
+            )
+
+        def new_grouped():
+            return stream.tile([P, CHUNKS, PACK * CHUNK], BF16, name="grouped", align_bytes=64)
+
+        def interleave_odd(grouped, odd, c):
+            nc.scalar.copy(
+                out=by_runs_interleaved(grouped[:, c, PACK * CHUNK // 2 :]),
+                in_=by_runs_of_planes(odd[:, :, c * CHUNK // 2 : (c + 1) * CHUNK // 2]),
+            )
+
+        def finish_even(grouped, square, first, end):
+            width = PACK * CHUNK // 2
+            for c in range(first, end):
+                nc.vector.tensor_scalar(
+                    out=grouped[:, c, :width],
+                    in0=square[:, c * width : (c + 1) * width],
+                    scalar1=2.0,
+                    scalar2=1.0,
+                    op0=ALU.mult,
+                    op1=ALU.subtract,
+                )
+
+        def quantise(grouped, first, end):
+            columns = (end - first) * CHUNK
+            codes = stream.tile([P, columns], U32, name="codes%d" % columns, align_bytes=64)
+            scales = stream.tile([P, columns], U8, name="scales%d" % columns, align_bytes=64)
+            nc.vector.quantize_mx(
+                out=codes[:].bitcast(FP8X4),
+                scales=scales[:],
+                in_=grouped[:, first:end, :].rearrange("p c k -> p (c k)"),
+            )
+            return codes, scales
+
+        def multiply(g, operand, first, sums):
+            codes, scales = operand
             for h in range(H_TILES):
                 nc.tensor.matmul_mx(
                     out=sums[h][:],
                     lhsT=w_words[:, g, P * PACK * h : P * PACK * (h + 1)].bitcast(FP8X4),
                     lhsT_scale=w_scales[:, g, P * h : P * (h + 1)],
-                    rhs=codes[:].bitcast(FP8X4),
-                    rhs_scale=scales[:],
+                    rhs=codes[:, first : first + CHUNK].bitcast(FP8X4),
+                    rhs_scale=scales[:, first : first + CHUNK],
                     start=(g == 0),
                     stop=(g == GROUPS - 1),
                 )
@@ -202,92 +236,73 @@ def tile_dlrkernel_e_kernel(tc, W_words, W_scales, Lambda_im, L, out):
             ]
 
         def store_bank(column, bank, h, strands, copy):
-            result = stream.tile([P, CHUNK], F32, name="result", bufs=CHUNKS * H_TILES)
+            result = stream.tile([P, CHUNK], F32, name="result", bufs=RESULTS)
             copy(
                 out=result[:].rearrange("p (r e) -> p r e", e=strands),
                 in_=bank[:].rearrange("p (e r) -> p r e", e=strands),
             )
             nc.sync.dma_start(out=out[0, P * h : P * (h + 1), column : column + CHUNK], in_=result[:])
 
-        def store_half(first_column, sums, strands):
-            for c in range(CHUNKS):
-                for h in range(H_TILES):
-                    copy = nc.scalar.copy if (c + h) % 2 == 0 else nc.vector.tensor_copy
-                    store_bank(first_column + CHUNK * c, sums[c][h], h, strands, copy)
-
         sums = open_banks()
-        take_short_steps(PARTS[0])
         grow_lower_half(0)
-        take_short_steps(PARTS[1])
+        squares = {}
+        odds = {}
         for g in range(GROUPS):
-            grouped = [stream.tile([P, PACK * CHUNK], BF16, name="grouped", align_bytes=64) for c in range(CHUNKS)]
+            grouped = new_grouped()
             for c in range(CHUNKS):
                 nc.scalar.copy(
-                    out=by_runs_interleaved(grouped[c][:]),
+                    out=by_runs_interleaved(grouped[:, c, :]),
                     in_=by_runs_of_planes(lower[:, PACK * g : PACK * (g + 1), CHUNK * c : CHUNK * (c + 1)]),
                 )
+            if g in EARLY_SQUARES:
+                early, c = EARLY_SQUARES[g]
+                if c == 0:
+                    squares[early] = new_squares()
+                make_squares(squares[early], early, c)
             if g + 1 < GROUPS:
                 grow_lower_half(g + 1)
             else:
-                square = squares_for_even_upper_columns(0)
-                odd = odd_upper_columns(0)
+                odds[0] = odd_upper_columns(0)
+            operand = quantise(grouped, 0, CHUNKS)
             for c in range(CHUNKS):
-                quantise_and_multiply(g, grouped[c], sums[c])
-
-        def new_grouped():
-            return [stream.tile([P, PACK * CHUNK], BF16, name="grouped", align_bytes=64) for c in range(CHUNKS)]
-
-        def interleave_odd(grouped, odd, c):
-            nc.scalar.copy(
-                out=by_runs_interleaved(grouped[c][:, PACK * CHUNK // 2 :]),
-                in_=by_runs_of_planes(odd[:, :, c * CHUNK // 2 : (c + 1) * CHUNK // 2]),
-            )
-
-        def finish_even(grouped, square, c):
-            nc.vector.tensor_scalar(
-                out=grouped[c][:, : PACK * CHUNK // 2],
-                in0=square[c][:],
-                scalar1=2.0,
-                scalar2=1.0,
-                op0=ALU.mult,
-                op1=ALU.subtract,
-            )
-
-        for g in range(GROUPS - 2):
-            grouped = new_grouped()
-            for c in range(CHUNKS):
-                interleave_odd(grouped, odd, c)
-            this_square = square
-            square = squares_for_even_upper_columns(g + 1)
-            odd = odd_upper_columns(g + 1)
-            for c in range(CHUNKS):
-                finish_even(grouped, this_square, c)
-            if g == 0:
-                store_half(0, sums, 1)
-                sums = open_banks()
-            for c in range(CHUNKS):
-                quantise_and_multiply(g, grouped[c], sums[c])
+                multiply(g, operand, CHUNK * c, sums[c])
 
         last = (GROUPS - 2, GROUPS - 1)
+        for g in range(last[0]):
+            grouped = new_grouped()
+            for c in range(CHUNKS):
+                interleave_odd(grouped, odds[g], c)
+            finish_even(grouped, squares[g], 0, CHUNKS)
+            squares[g + 2] = new_squares()
+            for c in range(CHUNKS):
+                make_squares(squares[g + 2], g + 2, c)
+            odds[g + 1] = odd_upper_columns(g + 1)
+            if g + 2 == last[1]:
+                odds[g + 2] = odd_upper_columns(g + 2)
+            if g == 0:
+                for c in range(CHUNKS):
+                    for h in range(H_TILES):
+                        copy = nc.scalar.copy if (c + h) % 2 == 0 else nc.vector.tensor_copy
+                        store_bank(CHUNK * c, sums[c][h], h, 1, copy)
+                sums = open_banks()
+            operand = quantise(grouped, 0, CHUNKS)
+            for c in range(CHUNKS):
+                multiply(g, operand, CHUNK * c, sums[c])
+
         grouped = {g: new_grouped() for g in last}
-        squares = {last[0]: square}
-        odds = {last[0]: odd}
-        interleave_odd(grouped[last[0]], odds[last[0]], 0)
-        squares[last[1]] = squares_for_even_upper_columns(last[1])
-        odds[last[1]] = odd_upper_columns(last[1])
-        interleave_odd(grouped[last[1]], odds[last[1]], 0)
-        interleave_odd(grouped[last[0]], odds[last[0]], 1)
-        interleave_odd(grouped[last[1]], odds[last[1]], 1)
+        for c in range(CHUNKS):
+            for g in last:
+                interleave_odd(grouped[g], odds[g], c)
         for g in last:
-            finish_even(grouped[g], squares[g], 0)
+            finish_even(grouped[g], squares[g], 0, 1)
         for g in last:
-            quantise_and_multiply(g, grouped[g][0], sums[0])
-        finish_even(grouped[last[0]], squares[last[0]], 1)
-        finish_even(grouped[last[1]], squares[last[1]], 1)
-        quantise_and_multiply(last[0], grouped[last[0]][1], sums[1])
+            multiply(g, quantise(grouped[g], 0, 1), 0, sums[0])
+        for g in last:
+            finish_even(grouped[g], squares[g], 1, 2)
+        multiply(last[0], quantise(grouped[last[0]], 1, 2), 0, sums[1])
         for h in range(H_TILES):
             store_bank(HALF, sums[0][h], h, 2, nc.scalar.copy)
-        quantise_and_multiply(last[1], grouped[last[1]][1], sums[1])
+        multiply(last[1], quantise(grouped[last[1]], 1, 2), 0, sums[1])
         for h in range(H_TILES):
             copy = nc.scalar.copy if h % 2 == 0 else nc.vector.tensor_copy
             store_bank(HALF + CHUNK, sums[1][h], h, 2, copy)

@@ -25,15 +25,17 @@ HALF = COLUMNS // 2
 CHUNK = 512
 CHUNKS = HALF // CHUNK
 RUN = 2
-PLANE = HALF + 4
+QUARTER = HALF // 2
+PITCH = QUARTER + 4
 SEED = 8
 STEPS = (8, 16, 32, 64, 128, 256, 512, 1024)
 SHORT_STEPS = 3
+FIRST_GROUPS = 2
 RESULTS = 8
 EARLY_SQUARES = {1: (0, 0), 2: (0, 1), 3: (1, 0), 4: (1, 1)}
 LOWER_STEPS = len(STEPS) - 1
 ARGS = SEED + len(STEPS) - 1
-PARTS = ((0, PLANES // 2), (PLANES // 2, PLANES))
+PARTS = ((0, GROUPS // 2), (GROUPS // 2, GROUPS))
 
 TWO_PI_HEAD = 6434.0 / 1024.0
 TWO_PI_TAIL = 2.0 * math.pi - TWO_PI_HEAD
@@ -70,11 +72,36 @@ def tile_dlrkernel_e_kernel(tc, W_words, W_scales, Lambda_im, L, out):
             out=w_words[:].bitcast(I32), in_=W_words.rearrange("g p h t -> p g (h t)").bitcast(I32)
         )
 
-        lower = keep.tile([P, PLANES, PLANE], F32)
-        twice_cos = keep.tile([P, PLANES, len(STEPS)], F32)
+        lower = keep.tile([P, GROUPS, 2, PACK, PITCH], F32)
+        twice_cos = keep.tile([P, GROUPS, PACK, len(STEPS)], F32)
+
+        def take_step(g, k):
+            step = STEPS[k]
+            for t in range(PACK):
+                nc.vector.scalar_tensor_tensor(
+                    out=lower[:, g, 0, t, step + 1 : 2 * step + 1],
+                    in0=lower[:, g, 0, t, 1 : step + 1],
+                    scalar=twice_cos[:, g, t, k : k + 1],
+                    in1=lower[:, g, 0, t, step - 1 :: -1],
+                    op0=ALU.mult,
+                    op1=ALU.subtract,
+                )
+
+        def grow_lower_half(g):
+            for k in range(SHORT_STEPS, LOWER_STEPS - 1):
+                take_step(g, k)
+            for t in range(PACK):
+                nc.vector.scalar_tensor_tensor(
+                    out=lower[:, g, 1, t, :QUARTER],
+                    in0=lower[:, g, 0, t, :QUARTER],
+                    scalar=twice_cos[:, g, t, LOWER_STEPS - 1 : LOWER_STEPS],
+                    in1=lower[:, g, 0, t, QUARTER:0:-1],
+                    op0=ALU.mult,
+                    op1=ALU.subtract,
+                )
 
         with tc.tile_pool(name="start", bufs=1) as start:
-            nc.vector.memset(lower[:, :, 0:1], 1.0)
+            nc.vector.memset(lower[:, :, 0, :, 0:1], 1.0)
             args = start.tile([P, ARGS], F32)
             for k, step in enumerate(STEPS[1:]):
                 nc.vector.memset(args[:, SEED + k : SEED + k + 1], float(step))
@@ -82,18 +109,17 @@ def tile_dlrkernel_e_kernel(tc, W_words, W_scales, Lambda_im, L, out):
             nc.gpsimd.iota(seed_positions[:], pattern=[[1, SEED]], base=1, channel_multiplier=0)
             nc.vector.tensor_copy(out=args[:, :SEED], in_=seed_positions[:])
             unused = start.tile([P, 1], F32)
-            nc.scalar.activation(out=unused[:], in_=lower[:, 0, 0:1], func=SIN)
-            lam_by_plane = lam[:].rearrange("p g t -> p (g t)")
+            nc.scalar.activation(out=unused[:], in_=lower[:, 0, 0, 0, 0:1], func=SIN)
 
-            shapes = [[P, end - first, ARGS] for first, end in PARTS]
+            shapes = [[P, (end - first) * PACK, ARGS] for first, end in PARTS]
             angles = [start.tile(shape, F32, name="angle%d" % i) for i, shape in enumerate(shapes)]
             periods = [start.tile(shape, I32, name="periods%d" % i) for i, shape in enumerate(shapes)]
-            cos_step = start.tile([P, PLANES, len(STEPS)], F32)
+            cos_step = start.tile([P, GROUPS, PACK, len(STEPS)], F32)
             for (first, end), shape, angle in zip(PARTS, shapes, angles):
                 nc.vector.tensor_tensor(
                     out=angle[:],
                     in0=args[:].unsqueeze(1).to_broadcast(shape),
-                    in1=lam_by_plane[:, first:end].unsqueeze(2).to_broadcast(shape),
+                    in1=lam[:, first:end].rearrange("p g t -> p (g t)").unsqueeze(2).to_broadcast(shape),
                     op=ALU.mult,
                 )
             for angle, period in zip(angles, periods):
@@ -106,82 +132,87 @@ def tile_dlrkernel_e_kernel(tc, W_words, W_scales, Lambda_im, L, out):
                         out=angle[:], in0=period[:], scalar=-share, in1=angle[:], op0=ALU.mult, op1=ALU.add
                     )
             for (first, end), angle in zip(PARTS, angles):
+                by_pass = angle[:].rearrange("p (g t) a -> p g t a", t=PACK)
                 nc.scalar.activation(out=angle[:], in_=angle[:], func=mybir.ActivationFunctionType.Abs)
                 nc.scalar.activation(
-                    out=cos_step[:, first:end, :], in_=angle[:, :, SEED - 1 :], func=SIN, bias=math.pi / 2, scale=-1.0
+                    out=cos_step[:, first:end], in_=by_pass[:, :, :, SEED - 1 :], func=SIN, bias=math.pi / 2, scale=-1.0
                 )
                 nc.scalar.activation(
-                    out=lower[:, first:end, 1 : SEED + 1],
-                    in_=angle[:, :, :SEED],
+                    out=lower[:, first:end, 0, :, 1 : SEED + 1],
+                    in_=by_pass[:, :, :, :SEED],
                     func=SIN,
                     bias=math.pi / 2,
                     scale=-1.0,
                 )
             for first, end in PARTS:
                 nc.vector.tensor_scalar(
-                    out=twice_cos[:, first:end, :],
-                    in0=cos_step[:, first:end, :],
-                    scalar1=2.0,
-                    scalar2=None,
-                    op0=ALU.mult,
+                    out=twice_cos[:, first:end], in0=cos_step[:, first:end], scalar1=2.0, scalar2=None, op0=ALU.mult
                 )
-            for k in range(SHORT_STEPS):
+
+            def subtract(product, first, end, step):
+                nc.vector.tensor_tensor(
+                    out=lower[:, first:end, 0, :, step + 1 : 2 * step + 1],
+                    in0=product[:],
+                    in1=lower[:, first:end, 0, :, step - 1 :: -1],
+                    op=ALU.subtract,
+                )
+
+            for k in range(SHORT_STEPS - 1):
                 step = STEPS[k]
-                shapes = [[P, end - first, step] for first, end in PARTS]
+                shapes = [[P, end - first, PACK, step] for first, end in PARTS]
                 products = [start.tile(shape, F32, name="product%d_%d" % (i, k)) for i, shape in enumerate(shapes)]
                 for (first, end), shape, product in zip(PARTS, shapes, products):
                     nc.vector.tensor_tensor(
                         out=product[:],
-                        in0=lower[:, first:end, 1 : step + 1],
-                        in1=twice_cos[:, first:end, k : k + 1].to_broadcast(shape),
+                        in0=lower[:, first:end, 0, :, 1 : step + 1],
+                        in1=twice_cos[:, first:end, :, k : k + 1].to_broadcast(shape),
                         op=ALU.mult,
                     )
                 for (first, end), product in zip(PARTS, products):
-                    nc.vector.tensor_tensor(
-                        out=lower[:, first:end, step + 1 : 2 * step + 1],
-                        in0=product[:],
-                        in1=lower[:, first:end, step - 1 :: -1],
-                        op=ALU.subtract,
+                    subtract(product, first, end, step)
+
+            k = SHORT_STEPS - 1
+            step = STEPS[k]
+            for g in range(FIRST_GROUPS):
+                take_step(g, k)
+            product = start.tile([P, GROUPS - FIRST_GROUPS, PACK, step], F32, name="product")
+            for g in range(FIRST_GROUPS, GROUPS):
+                for t in range(PACK):
+                    nc.scalar.activation(
+                        out=product[:, g - FIRST_GROUPS, t, :],
+                        in_=lower[:, g, 0, t, 1 : step + 1],
+                        func=mybir.ActivationFunctionType.Copy,
+                        scale=twice_cos[:, g, t, k : k + 1],
                     )
+            grow_lower_half(0)
+            subtract(product, FIRST_GROUPS, GROUPS, step)
 
         upper = stack.enter_context(tc.tile_pool(name="upper", bufs=2))
 
-        def grow_lower_half(g):
-            for k in range(SHORT_STEPS, LOWER_STEPS):
-                step = STEPS[k]
-                for q in range(PACK * g, PACK * (g + 1)):
-                    nc.vector.scalar_tensor_tensor(
-                        out=lower[:, q, step + 1 : 2 * step + 1],
-                        in0=lower[:, q, 1 : step + 1],
-                        scalar=twice_cos[:, q, k : k + 1],
-                        in1=lower[:, q, step - 1 :: -1],
-                        op0=ALU.mult,
-                        op1=ALU.subtract,
-                    )
+        def new_odd():
+            return upper.tile([P, PACK, HALF // 2], BF16, name="odd")
 
-        def odd_upper_columns(g):
-            odd = upper.tile([P, PACK, HALF // 2], BF16, bufs=3)
+        def make_odd(odd, g, first, end):
             for t in range(PACK):
-                q = PACK * g + t
+                columns = lower[:, g, :, t, 1:QUARTER:2]
                 nc.vector.scalar_tensor_tensor(
-                    out=odd[:, t, :],
-                    in0=lower[:, q, 1:HALF:2],
-                    scalar=twice_cos[:, q, LOWER_STEPS : LOWER_STEPS + 1],
-                    in1=lower[:, q, HALF - 1 : 0 : -2],
+                    out=odd[:, t, :].rearrange("p (b r) -> p b r", b=2)[:, first:end],
+                    in0=columns[:, first:end],
+                    scalar=twice_cos[:, g, t, LOWER_STEPS : LOWER_STEPS + 1],
+                    in1=columns[:, ::-1, ::-1][:, first:end],
                     op0=ALU.mult,
                     op1=ALU.subtract,
                 )
-            return odd
 
         def new_squares():
             return upper.tile([P, PACK * HALF // 2], F32, name="square")
 
         def make_squares(square, g, c):
             width = PACK * CHUNK // 2
-            first = (HALF + c * CHUNK) // 2
+            first = c * CHUNK // 2
             nc.scalar.square(
                 out=by_runs_interleaved(square[:, c * width : (c + 1) * width]),
-                in_=by_runs_of_planes(lower[:, PACK * g : PACK * (g + 1), first : first + CHUNK // 2]),
+                in_=by_runs_of_planes(lower[:, g, 1, :, first : first + CHUNK // 2]),
             )
 
         def new_grouped():
@@ -207,8 +238,9 @@ def tile_dlrkernel_e_kernel(tc, W_words, W_scales, Lambda_im, L, out):
 
         def quantise(grouped, first, end):
             columns = (end - first) * CHUNK
-            codes = stream.tile([P, columns], U32, name="codes%d" % columns, align_bytes=64)
-            scales = stream.tile([P, columns], U8, name="scales%d" % columns, align_bytes=64)
+            slots = 2 * CHUNKS * CHUNK // columns
+            codes = stream.tile([P, columns], U32, name="codes%d" % columns, bufs=slots, align_bytes=64)
+            scales = stream.tile([P, columns], U8, name="scales%d" % columns, bufs=slots, align_bytes=64)
             nc.vector.quantize_mx(
                 out=codes[:].bitcast(FP8X4),
                 scales=scales[:],
@@ -244,7 +276,6 @@ def tile_dlrkernel_e_kernel(tc, W_words, W_scales, Lambda_im, L, out):
             nc.sync.dma_start(out=out[0, P * h : P * (h + 1), column : column + CHUNK], in_=result[:])
 
         sums = open_banks()
-        grow_lower_half(0)
         squares = {}
         odds = {}
         for g in range(GROUPS):
@@ -252,7 +283,7 @@ def tile_dlrkernel_e_kernel(tc, W_words, W_scales, Lambda_im, L, out):
             for c in range(CHUNKS):
                 nc.scalar.copy(
                     out=by_runs_interleaved(grouped[:, c, :]),
-                    in_=by_runs_of_planes(lower[:, PACK * g : PACK * (g + 1), CHUNK * c : CHUNK * (c + 1)]),
+                    in_=by_runs_of_planes(lower[:, g, c, :, :CHUNK]),
                 )
             if g in EARLY_SQUARES:
                 early, c = EARLY_SQUARES[g]
@@ -262,7 +293,8 @@ def tile_dlrkernel_e_kernel(tc, W_words, W_scales, Lambda_im, L, out):
             if g + 1 < GROUPS:
                 grow_lower_half(g + 1)
             else:
-                odds[0] = odd_upper_columns(0)
+                odds[0] = new_odd()
+                make_odd(odds[0], 0, 0, CHUNKS)
             operand = quantise(grouped, 0, CHUNKS)
             for c in range(CHUNKS):
                 multiply(g, operand, CHUNK * c, sums[c])
@@ -276,13 +308,12 @@ def tile_dlrkernel_e_kernel(tc, W_words, W_scales, Lambda_im, L, out):
             squares[g + 2] = new_squares()
             for c in range(CHUNKS):
                 make_squares(squares[g + 2], g + 2, c)
-            odds[g + 1] = odd_upper_columns(g + 1)
-            if g + 2 == last[1]:
-                odds[g + 2] = odd_upper_columns(g + 2)
+            odds[g + 1] = new_odd()
+            make_odd(odds[g + 1], g + 1, 0, CHUNKS)
             if g == 0:
                 for c in range(CHUNKS):
                     for h in range(H_TILES):
-                        copy = nc.scalar.copy if (c + h) % 2 == 0 else nc.vector.tensor_copy
+                        copy = nc.vector.tensor_copy if h == 0 else nc.scalar.copy
                         store_bank(CHUNK * c, sums[c][h], h, 1, copy)
                 sums = open_banks()
             operand = quantise(grouped, 0, CHUNKS)
@@ -290,19 +321,21 @@ def tile_dlrkernel_e_kernel(tc, W_words, W_scales, Lambda_im, L, out):
                 multiply(g, operand, CHUNK * c, sums[c])
 
         grouped = {g: new_grouped() for g in last}
-        for c in range(CHUNKS):
-            for g in last:
-                interleave_odd(grouped[g], odds[g], c)
+        odds[last[1]] = new_odd()
+        make_odd(odds[last[1]], last[1], 0, 1)
+        for g in last:
+            interleave_odd(grouped[g], odds[g], 0)
+        interleave_odd(grouped[last[0]], odds[last[0]], 1)
         for g in last:
             finish_even(grouped[g], squares[g], 0, 1)
-        for g in last:
             multiply(g, quantise(grouped[g], 0, 1), 0, sums[0])
-        for g in last:
-            finish_even(grouped[g], squares[g], 1, 2)
-        multiply(last[0], quantise(grouped[last[0]], 1, 2), 0, sums[1])
+        make_odd(odds[last[1]], last[1], 1, 2)
+        interleave_odd(grouped[last[1]], odds[last[1]], 1)
         for h in range(H_TILES):
             store_bank(HALF, sums[0][h], h, 2, nc.scalar.copy)
-        multiply(last[1], quantise(grouped[last[1]], 1, 2), 0, sums[1])
+        for g in last:
+            finish_even(grouped[g], squares[g], 1, 2)
+            multiply(g, quantise(grouped[g], 1, 2), 0, sums[1])
         for h in range(H_TILES):
-            copy = nc.scalar.copy if h % 2 == 0 else nc.vector.tensor_copy
+            copy = nc.vector.tensor_copy if h < H_TILES // 2 else nc.scalar.copy
             store_bank(HALF + CHUNK, sums[1][h], h, 2, copy)

@@ -25,17 +25,17 @@ HALF = COLUMNS // 2
 CHUNK = 512
 CHUNKS = HALF // CHUNK
 RUN = 2
-QUARTER = HALF // 2
-PITCH = QUARTER + 4
+BLOCK = HALF // 4
+BASE = 64
+ODD = BASE // 2 + 4
+ROW = ODD + BLOCK
 SEED = 8
 STEPS = (8, 16, 32, 64, 128, 256, 512, 1024)
 SHORT_STEPS = 3
-FIRST_GROUPS = 2
+FIRST_PLANES = 8
 RESULTS = 8
-EARLY_SQUARES = {1: (0, 0), 2: (0, 1), 3: (1, 0), 4: (1, 1)}
-LOWER_STEPS = len(STEPS) - 1
-ARGS = SEED + len(STEPS) - 1
-PARTS = ((0, GROUPS // 2), (GROUPS // 2, GROUPS))
+ARGS = SEED + len(STEPS)
+PARTS = ((0, PLANES // 2), (PLANES // 2, PLANES))
 
 TWO_PI_HEAD = 6434.0 / 1024.0
 TWO_PI_TAIL = 2.0 * math.pi - TWO_PI_HEAD
@@ -45,8 +45,16 @@ def by_runs_of_planes(planes):
     return planes.rearrange("p t (c i) -> p c t i", i=RUN)
 
 
-def by_runs_interleaved(grouped):
-    return grouped.rearrange("p (c i t) -> p c t i", i=RUN, t=PACK)
+def by_runs_interleaved(columns):
+    return columns.rearrange("p (c i) t -> p c t i", i=RUN)
+
+
+def rising(rows):
+    return rows[:, :, 1 : 2 * ODD - 1].rearrange("p q (e i) -> p q e i", e=2)
+
+
+def from_zero(rows):
+    return rows[:, :, : 2 * ODD].rearrange("p q (e i) -> p q e i", e=2)
 
 
 def tile_dlrkernel_e_kernel(tc, W_words, W_scales, Lambda_im, L, out):
@@ -72,54 +80,50 @@ def tile_dlrkernel_e_kernel(tc, W_words, W_scales, Lambda_im, L, out):
             out=w_words[:].bitcast(I32), in_=W_words.rearrange("g p h t -> p g (h t)").bitcast(I32)
         )
 
-        lower = keep.tile([P, GROUPS, 2, PACK, PITCH], F32)
-        twice_cos = keep.tile([P, GROUPS, PACK, len(STEPS)], F32)
+        lower = keep.tile([P, 2, PLANES, ROW], F32)
+        twice_cos = keep.tile([P, PLANES, len(STEPS)], F32)
+        square = keep.tile([P, GROUPS, HALF // 2, PACK], F32)
 
         def take_step(g, k):
-            step = STEPS[k]
-            for t in range(PACK):
+            half = STEPS[k] // 2
+            for q in range(PACK * g, PACK * (g + 1)):
                 nc.vector.scalar_tensor_tensor(
-                    out=lower[:, g, 0, t, step + 1 : 2 * step + 1],
-                    in0=lower[:, g, 0, t, 1 : step + 1],
-                    scalar=twice_cos[:, g, t, k : k + 1],
-                    in1=lower[:, g, 0, t, step - 1 :: -1],
+                    out=lower[:, 0, q, ODD + half : ODD + 2 * half] if half < BLOCK else lower[:, 1, q, ODD:],
+                    in0=lower[:, 0, q, ODD : ODD + half],
+                    scalar=twice_cos[:, q, k : k + 1],
+                    in1=lower[:, 0, q, ODD : ODD + half][:, ::-1],
                     op0=ALU.mult,
                     op1=ALU.subtract,
                 )
 
-        def grow_lower_half(g):
-            for k in range(SHORT_STEPS, LOWER_STEPS - 1):
+        def grow_first_block(g):
+            for k in range(SHORT_STEPS, len(STEPS) - 2):
                 take_step(g, k)
-            for t in range(PACK):
-                nc.vector.scalar_tensor_tensor(
-                    out=lower[:, g, 1, t, :QUARTER],
-                    in0=lower[:, g, 0, t, :QUARTER],
-                    scalar=twice_cos[:, g, t, LOWER_STEPS - 1 : LOWER_STEPS],
-                    in1=lower[:, g, 0, t, QUARTER:0:-1],
-                    op0=ALU.mult,
-                    op1=ALU.subtract,
-                )
+
+        def grow_second_block(g):
+            take_step(g, len(STEPS) - 2)
 
         with tc.tile_pool(name="start", bufs=1) as start:
-            nc.vector.memset(lower[:, :, 0, :, 0:1], 1.0)
+            nc.vector.memset(lower[:, 0, :, 0:1], 1.0)
             args = start.tile([P, ARGS], F32)
-            for k, step in enumerate(STEPS[1:]):
+            for k, step in enumerate(STEPS):
                 nc.vector.memset(args[:, SEED + k : SEED + k + 1], float(step))
-            seed_positions = start.tile([P, SEED], I32)
-            nc.gpsimd.iota(seed_positions[:], pattern=[[1, SEED]], base=1, channel_multiplier=0)
-            nc.vector.tensor_copy(out=args[:, :SEED], in_=seed_positions[:])
+            seed_positions = start.tile([P, 2, SEED // 2], I32)
+            nc.gpsimd.iota(seed_positions[:], pattern=[[-1, 2], [2, SEED // 2]], base=2, channel_multiplier=0)
+            nc.vector.tensor_copy(out=args[:, :SEED], in_=seed_positions[:].rearrange("p e i -> p (e i)"))
             unused = start.tile([P, 1], F32)
-            nc.scalar.activation(out=unused[:], in_=lower[:, 0, 0, 0, 0:1], func=SIN)
+            nc.scalar.activation(out=unused[:], in_=lower[:, 0, 0, 0:1], func=SIN)
 
-            shapes = [[P, (end - first) * PACK, ARGS] for first, end in PARTS]
+            lam_by_plane = lam[:].rearrange("p g t -> p (g t)")
+            shapes = [[P, end - first, ARGS] for first, end in PARTS]
             angles = [start.tile(shape, F32, name="angle%d" % i) for i, shape in enumerate(shapes)]
             periods = [start.tile(shape, I32, name="periods%d" % i) for i, shape in enumerate(shapes)]
-            cos_step = start.tile([P, GROUPS, PACK, len(STEPS)], F32)
+            cos_step = start.tile([P, PLANES, len(STEPS)], F32)
             for (first, end), shape, angle in zip(PARTS, shapes, angles):
                 nc.vector.tensor_tensor(
                     out=angle[:],
                     in0=args[:].unsqueeze(1).to_broadcast(shape),
-                    in1=lam[:, first:end].rearrange("p g t -> p (g t)").unsqueeze(2).to_broadcast(shape),
+                    in1=lam_by_plane[:, first:end].unsqueeze(2).to_broadcast(shape),
                     op=ALU.mult,
                 )
             for angle, period in zip(angles, periods):
@@ -132,14 +136,13 @@ def tile_dlrkernel_e_kernel(tc, W_words, W_scales, Lambda_im, L, out):
                         out=angle[:], in0=period[:], scalar=-share, in1=angle[:], op0=ALU.mult, op1=ALU.add
                     )
             for (first, end), angle in zip(PARTS, angles):
-                by_pass = angle[:].rearrange("p (g t) a -> p g t a", t=PACK)
                 nc.scalar.activation(out=angle[:], in_=angle[:], func=mybir.ActivationFunctionType.Abs)
                 nc.scalar.activation(
-                    out=cos_step[:, first:end], in_=by_pass[:, :, :, SEED - 1 :], func=SIN, bias=math.pi / 2, scale=-1.0
+                    out=cos_step[:, first:end], in_=angle[:, :, SEED:], func=SIN, bias=math.pi / 2, scale=-1.0
                 )
                 nc.scalar.activation(
-                    out=lower[:, first:end, 0, :, 1 : SEED + 1],
-                    in_=by_pass[:, :, :, :SEED],
+                    out=rising(lower[:, 0, first:end])[:, :, :, : SEED // 2],
+                    in_=angle[:, :, :SEED].rearrange("p q (e i) -> p q e i", e=2),
                     func=SIN,
                     bias=math.pi / 2,
                     scale=-1.0,
@@ -149,92 +152,118 @@ def tile_dlrkernel_e_kernel(tc, W_words, W_scales, Lambda_im, L, out):
                     out=twice_cos[:, first:end], in0=cos_step[:, first:end], scalar1=2.0, scalar2=None, op0=ALU.mult
                 )
 
-            def subtract(product, first, end, step):
+            def subtract(product, first, end, half):
+                rows = lower[:, 0, first:end]
                 nc.vector.tensor_tensor(
-                    out=lower[:, first:end, 0, :, step + 1 : 2 * step + 1],
+                    out=rising(rows)[:, :, :, half : 2 * half],
                     in0=product[:],
-                    in1=lower[:, first:end, 0, :, step - 1 :: -1],
+                    in1=from_zero(rows)[:, :, :, half - 1 :: -1],
                     op=ALU.subtract,
                 )
 
             for k in range(SHORT_STEPS - 1):
-                step = STEPS[k]
-                shapes = [[P, end - first, PACK, step] for first, end in PARTS]
+                half = STEPS[k] // 2
+                shapes = [[P, end - first, 2, half] for first, end in PARTS]
                 products = [start.tile(shape, F32, name="product%d_%d" % (i, k)) for i, shape in enumerate(shapes)]
                 for (first, end), shape, product in zip(PARTS, shapes, products):
                     nc.vector.tensor_tensor(
                         out=product[:],
-                        in0=lower[:, first:end, 0, :, 1 : step + 1],
-                        in1=twice_cos[:, first:end, :, k : k + 1].to_broadcast(shape),
+                        in0=rising(lower[:, 0, first:end])[:, :, :, :half],
+                        in1=twice_cos[:, first:end, k : k + 1].unsqueeze(3).to_broadcast(shape),
                         op=ALU.mult,
                     )
                 for (first, end), product in zip(PARTS, products):
-                    subtract(product, first, end, step)
+                    subtract(product, first, end, half)
 
             k = SHORT_STEPS - 1
-            step = STEPS[k]
-            for g in range(FIRST_GROUPS):
-                take_step(g, k)
-            product = start.tile([P, GROUPS - FIRST_GROUPS, PACK, step], F32, name="product")
-            for g in range(FIRST_GROUPS, GROUPS):
-                for t in range(PACK):
-                    nc.scalar.activation(
-                        out=product[:, g - FIRST_GROUPS, t, :],
-                        in_=lower[:, g, 0, t, 1 : step + 1],
-                        func=mybir.ActivationFunctionType.Copy,
-                        scale=twice_cos[:, g, t, k : k + 1],
-                    )
-            grow_lower_half(0)
-            subtract(product, FIRST_GROUPS, GROUPS, step)
+            half = STEPS[k] // 2
+            up, down = rising(lower[:, 0]), from_zero(lower[:, 0])
+            for q in range(FIRST_PLANES):
+                nc.vector.scalar_tensor_tensor(
+                    out=up[:, q, :, half : 2 * half],
+                    in0=up[:, q, :, :half],
+                    scalar=twice_cos[:, q, k : k + 1],
+                    in1=down[:, q, :, half - 1 :: -1],
+                    op0=ALU.mult,
+                    op1=ALU.subtract,
+                )
+            product = start.tile([P, PLANES - FIRST_PLANES, 2, half], F32, name="product")
+            for q in range(FIRST_PLANES, PLANES):
+                nc.scalar.activation(
+                    out=product[:, q - FIRST_PLANES],
+                    in_=up[:, q, :, :half],
+                    func=mybir.ActivationFunctionType.Copy,
+                    scale=twice_cos[:, q, k : k + 1],
+                )
+            grow_first_block(0)
+            grow_second_block(0)
+            subtract(product, FIRST_PLANES, PLANES, half)
 
         upper = stack.enter_context(tc.tile_pool(name="upper", bufs=2))
 
-        def new_odd():
-            return upper.tile([P, PACK, HALF // 2], BF16, name="odd")
+        def planes_of(g):
+            return slice(PACK * g, PACK * (g + 1))
 
-        def make_odd(odd, g, first, end):
+        def square_first_block(g):
+            nc.scalar.square(
+                out=by_runs_interleaved(square[:, g, 1::2, :]),
+                in_=by_runs_of_planes(lower[:, 0, planes_of(g), ODD:]),
+            )
+            nc.scalar.square(
+                out=by_runs_interleaved(square[:, g, 0:BASE:2, :]),
+                in_=by_runs_of_planes(lower[:, 0, planes_of(g), : BASE // 2]),
+            )
+
+        def square_again(out, g, first):
+            nc.scalar.activation(
+                out=out,
+                in_=square[:, g, first // 2 : first, :],
+                func=mybir.ActivationFunctionType.Square,
+                scale=2.0,
+                bias=-1.0,
+            )
+
+        def square_evens(g, first):
+            square_again(square[:, g, first : 2 * first : 2, :], g, first)
+
+        def square_second_block(g):
+            high = upper.tile([P, HALF // 2, PACK], F32, name="high")
+            nc.scalar.square(
+                out=by_runs_interleaved(high[:, 1::2, :]),
+                in_=by_runs_of_planes(lower[:, 1, planes_of(g), ODD:]),
+            )
+            square_again(high[:, 0::2, :], g, HALF // 2)
+            return high
+
+        def make_odd(g):
+            odd = upper.tile([P, PACK, HALF // 2], BF16, name="odd")
             for t in range(PACK):
-                columns = lower[:, g, :, t, 1:QUARTER:2]
+                q = PACK * g + t
                 nc.vector.scalar_tensor_tensor(
-                    out=odd[:, t, :].rearrange("p (b r) -> p b r", b=2)[:, first:end],
-                    in0=columns[:, first:end],
-                    scalar=twice_cos[:, g, t, LOWER_STEPS : LOWER_STEPS + 1],
-                    in1=columns[:, ::-1, ::-1][:, first:end],
+                    out=odd[:, t, :].rearrange("p (b r) -> p b r", b=2),
+                    in0=lower[:, :, q, ODD:],
+                    scalar=twice_cos[:, q, len(STEPS) - 1 :],
+                    in1=lower[:, :, q, ODD:][:, ::-1, ::-1],
                     op0=ALU.mult,
                     op1=ALU.subtract,
                 )
-
-        def new_squares():
-            return upper.tile([P, PACK * HALF // 2], F32, name="square")
-
-        def make_squares(square, g, c):
-            width = PACK * CHUNK // 2
-            first = c * CHUNK // 2
-            nc.scalar.square(
-                out=by_runs_interleaved(square[:, c * width : (c + 1) * width]),
-                in_=by_runs_of_planes(lower[:, g, 1, :, first : first + CHUNK // 2]),
-            )
+            return odd
 
         def new_grouped():
-            return stream.tile([P, CHUNKS, PACK * CHUNK], BF16, name="grouped", align_bytes=64)
+            return stream.tile([P, CHUNKS, 2, CHUNK // 2, PACK], BF16, name="grouped", align_bytes=64)
 
         def interleave_odd(grouped, odd, c):
-            nc.scalar.copy(
-                out=by_runs_interleaved(grouped[:, c, PACK * CHUNK // 2 :]),
-                in_=by_runs_of_planes(odd[:, :, c * CHUNK // 2 : (c + 1) * CHUNK // 2]),
-            )
+            nc.scalar.copy(out=by_runs_interleaved(grouped[:, c, 1]), in_=by_runs_of_planes(odd))
 
-        def finish_even(grouped, square, first, end):
-            width = PACK * CHUNK // 2
-            for c in range(first, end):
-                nc.vector.tensor_scalar(
-                    out=grouped[:, c, :width],
-                    in0=square[:, c * width : (c + 1) * width],
-                    scalar1=2.0,
-                    scalar2=1.0,
-                    op0=ALU.mult,
-                    op1=ALU.subtract,
-                )
+        def finish_even(grouped, squares, c):
+            nc.vector.tensor_scalar(
+                out=grouped[:, c, 0],
+                in0=squares[:, c * CHUNK // 2 : (c + 1) * CHUNK // 2, :],
+                scalar1=2.0,
+                scalar2=1.0,
+                op0=ALU.mult,
+                op1=ALU.subtract,
+            )
 
         def quantise(grouped, first, end):
             columns = (end - first) * CHUNK
@@ -244,7 +273,7 @@ def tile_dlrkernel_e_kernel(tc, W_words, W_scales, Lambda_im, L, out):
             nc.vector.quantize_mx(
                 out=codes[:].bitcast(FP8X4),
                 scales=scales[:],
-                in_=grouped[:, first:end, :].rearrange("p c k -> p (c k)"),
+                in_=grouped[:, first:end].rearrange("p c e l t -> p (c e l t)"),
             )
             return codes, scales
 
@@ -267,75 +296,89 @@ def tile_dlrkernel_e_kernel(tc, W_words, W_scales, Lambda_im, L, out):
                 for c in range(CHUNKS)
             ]
 
-        def store_bank(column, bank, h, strands, copy):
+        def store_bank(column, bank, h, copy):
             result = stream.tile([P, CHUNK], F32, name="result", bufs=RESULTS)
             copy(
-                out=result[:].rearrange("p (r e) -> p r e", e=strands),
-                in_=bank[:].rearrange("p (e r) -> p r e", e=strands),
+                out=result[:].rearrange("p (r e) -> p r e", e=2),
+                in_=bank[:].rearrange("p (e r) -> p r e", e=2),
             )
             nc.sync.dma_start(out=out[0, P * h : P * (h + 1), column : column + CHUNK], in_=result[:])
 
         sums = open_banks()
-        squares = {}
         odds = {}
+        highs = {}
+        grow_first_block(1)
+        grow_second_block(1)
+        square_first_block(0)
+        for first in (64, 128, 256):
+            square_evens(0, first)
         for g in range(GROUPS):
             grouped = new_grouped()
-            for c in range(CHUNKS):
-                nc.scalar.copy(
-                    out=by_runs_interleaved(grouped[:, c, :]),
-                    in_=by_runs_of_planes(lower[:, g, c, :, :CHUNK]),
-                )
-            if g in EARLY_SQUARES:
-                early, c = EARLY_SQUARES[g]
-                if c == 0:
-                    squares[early] = new_squares()
-                make_squares(squares[early], early, c)
             if g + 1 < GROUPS:
-                grow_lower_half(g + 1)
+                square_first_block(g + 1)
             else:
-                odds[0] = new_odd()
-                make_odd(odds[0], 0, 0, CHUNKS)
+                highs[0] = square_second_block(0)
+            if g > 0:
+                square_evens(g, 256)
+            interleave_odd(grouped, lower[:, 0, planes_of(g), ODD:], 0)
+            if g + 1 < GROUPS:
+                square_evens(g + 1, 64)
+            interleave_odd(grouped, lower[:, 1, planes_of(g), ODD:], 1)
+            if g + 1 < GROUPS:
+                square_evens(g + 1, 128)
+
+            if g + 2 < GROUPS:
+                grow_first_block(g + 2)
+            for c in range(CHUNKS):
+                finish_even(grouped, square[:, g], c)
+            if g + 2 < GROUPS:
+                grow_second_block(g + 2)
+            else:
+                odds[g + 2 - GROUPS] = make_odd(g + 2 - GROUPS)
             operand = quantise(grouped, 0, CHUNKS)
             for c in range(CHUNKS):
                 multiply(g, operand, CHUNK * c, sums[c])
+
+        def interleave_upper(grouped, g, c):
+            interleave_odd(grouped, odds[g][:, :, c * CHUNK // 2 : (c + 1) * CHUNK // 2], c)
 
         last = (GROUPS - 2, GROUPS - 1)
         for g in range(last[0]):
             grouped = new_grouped()
             for c in range(CHUNKS):
-                interleave_odd(grouped, odds[g], c)
-            finish_even(grouped, squares[g], 0, CHUNKS)
-            squares[g + 2] = new_squares()
+                interleave_upper(grouped, g, c)
+            highs[g + 1] = square_second_block(g + 1)
             for c in range(CHUNKS):
-                make_squares(squares[g + 2], g + 2, c)
-            odds[g + 1] = new_odd()
-            make_odd(odds[g + 1], g + 1, 0, CHUNKS)
+                finish_even(grouped, highs[g], c)
             if g == 0:
                 for c in range(CHUNKS):
                     for h in range(H_TILES):
-                        copy = nc.vector.tensor_copy if h == 0 else nc.scalar.copy
-                        store_bank(CHUNK * c, sums[c][h], h, 1, copy)
+                        copy = nc.vector.tensor_copy if h % 2 == 0 else nc.scalar.copy
+                        store_bank(CHUNK * c, sums[c][h], h, copy)
                 sums = open_banks()
+            if g + 2 < last[1]:
+                odds[g + 2] = make_odd(g + 2)
             operand = quantise(grouped, 0, CHUNKS)
             for c in range(CHUNKS):
                 multiply(g, operand, CHUNK * c, sums[c])
+        odds[last[1]] = make_odd(last[1])
 
         grouped = {g: new_grouped() for g in last}
-        odds[last[1]] = new_odd()
-        make_odd(odds[last[1]], last[1], 0, 1)
+        interleave_upper(grouped[last[0]], last[0], 0)
+        highs[last[1]] = square_second_block(last[1])
+        interleave_upper(grouped[last[1]], last[1], 0)
         for g in last:
-            interleave_odd(grouped[g], odds[g], 0)
-        interleave_odd(grouped[last[0]], odds[last[0]], 1)
+            interleave_upper(grouped[g], g, 1)
         for g in last:
-            finish_even(grouped[g], squares[g], 0, 1)
+            finish_even(grouped[g], highs[g], 0)
+        for g in last:
             multiply(g, quantise(grouped[g], 0, 1), 0, sums[0])
-        make_odd(odds[last[1]], last[1], 1, 2)
-        interleave_odd(grouped[last[1]], odds[last[1]], 1)
         for h in range(H_TILES):
-            store_bank(HALF, sums[0][h], h, 2, nc.scalar.copy)
+            store_bank(HALF, sums[0][h], h, nc.scalar.copy)
         for g in last:
-            finish_even(grouped[g], squares[g], 1, 2)
+            finish_even(grouped[g], highs[g], 1)
+        for g in last:
             multiply(g, quantise(grouped[g], 1, 2), 0, sums[1])
         for h in range(H_TILES):
             copy = nc.vector.tensor_copy if h < H_TILES // 2 else nc.scalar.copy
-            store_bank(HALF + CHUNK, sums[1][h], h, 2, copy)
+            store_bank(HALF + CHUNK, sums[1][h], h, copy)

@@ -21,11 +21,12 @@ PLANES = GROUPS * PACK
 H = 512
 H_TILES = H // P
 COLUMNS = 2048
-HALF = COLUMNS // 2
 CHUNK = 512
-CHUNKS = HALF // CHUNK
+SWEEPS = COLUMNS // CHUNK
+UNITS = SWEEPS * GROUPS
+AHEAD = 3
 RUN = 2
-BLOCK = HALF // 4
+BLOCK = CHUNK // 2
 BASE = 64
 ODD = BASE // 2 + 4
 ROW = ODD + BLOCK
@@ -33,7 +34,7 @@ SEED = 8
 STEPS = (8, 16, 32, 64, 128, 256, 512, 1024)
 SHORT_STEPS = 3
 FIRST_PLANES = 8
-RESULTS = 8
+EVEN_STAGES = (64, 128)
 ARGS = SEED + len(STEPS)
 PARTS = ((0, PLANES // 2), (PLANES // 2, PLANES))
 
@@ -63,7 +64,7 @@ def tile_dlrkernel_e_kernel(tc, W_words, W_scales, Lambda_im, L, out):
     with ExitStack() as stack:
         stack.enter_context(tc.manual_schedule())
         keep = stack.enter_context(tc.tile_pool(name="keep", bufs=1))
-        stream = stack.enter_context(tc.tile_pool(name="stream", bufs=2))
+        stream = stack.enter_context(tc.tile_pool(name="stream", bufs=4))
         banks = stack.enter_context(tc.psum_pool(name="banks", bufs=1))
 
         lam = keep.tile([P, GROUPS, PACK], BF16)
@@ -82,7 +83,7 @@ def tile_dlrkernel_e_kernel(tc, W_words, W_scales, Lambda_im, L, out):
 
         lower = keep.tile([P, 2, PLANES, ROW], F32)
         twice_cos = keep.tile([P, PLANES, len(STEPS)], F32)
-        square = keep.tile([P, GROUPS, HALF // 2, PACK], F32)
+        square = keep.tile([P, GROUPS, 2 * BLOCK, PACK], F32)
 
         def take_step(g, k):
             half = STEPS[k] // 2
@@ -196,189 +197,134 @@ def tile_dlrkernel_e_kernel(tc, W_words, W_scales, Lambda_im, L, out):
                     scale=twice_cos[:, q, k : k + 1],
                 )
             grow_first_block(0)
-            grow_second_block(0)
             subtract(product, FIRST_PLANES, PLANES, half)
 
-        upper = stack.enter_context(tc.tile_pool(name="upper", bufs=2))
+        odds = {}
+        squares = {}
+        grouped = {}
+        sums = {}
 
         def planes_of(g):
             return slice(PACK * g, PACK * (g + 1))
 
-        def square_first_block(g):
-            nc.scalar.square(
-                out=by_runs_interleaved(square[:, g, 1::2, :]),
-                in_=by_runs_of_planes(lower[:, 0, planes_of(g), ODD:]),
-            )
-            nc.scalar.square(
-                out=by_runs_interleaved(square[:, g, 0:BASE:2, :]),
-                in_=by_runs_of_planes(lower[:, 0, planes_of(g), : BASE // 2]),
-            )
+        def grow(unit):
+            sweep, g = divmod(unit, GROUPS)
+            if sweep == 0:
+                if g > 0:
+                    grow_first_block(g)
+                odds[unit] = lower[:, 0, planes_of(g), ODD:]
+            elif sweep == 1:
+                grow_second_block(g)
+                odds[unit] = lower[:, 1, planes_of(g), ODD:]
+            else:
+                odd = stream.tile([P, PACK, BLOCK], BF16, name="odd")
+                for t in range(PACK):
+                    q = PACK * g + t
+                    nc.vector.scalar_tensor_tensor(
+                        out=odd[:, t, :],
+                        in0=lower[:, sweep - 2, q, ODD:],
+                        scalar=twice_cos[:, q, len(STEPS) - 1 :],
+                        in1=lower[:, 3 - sweep, q, ODD:][:, ::-1],
+                        op0=ALU.mult,
+                        op1=ALU.subtract,
+                    )
+                odds[unit] = odd[:]
 
-        def square_again(out, g, first):
+        def square_planes(out, planes):
+            nc.scalar.square(out=by_runs_interleaved(out), in_=by_runs_of_planes(planes))
+
+        def square_again(out, halves):
             nc.scalar.activation(
-                out=out,
-                in_=square[:, g, first // 2 : first, :],
-                func=mybir.ActivationFunctionType.Square,
-                scale=2.0,
-                bias=-1.0,
+                out=out, in_=halves, func=mybir.ActivationFunctionType.Square, scale=2.0, bias=-1.0
             )
 
-        def square_evens(g, first):
-            square_again(square[:, g, first : 2 * first : 2, :], g, first)
+        def interleave(unit):
+            sweep, g = divmod(unit, GROUPS)
+            own = square[:, g]
+            columns = stream.tile([P, 2, BLOCK, PACK], BF16, name="columns", align_bytes=64)
+            grouped[unit] = columns
 
-        def square_second_block(g):
-            high = upper.tile([P, HALF // 2, PACK], F32, name="high")
-            nc.scalar.square(
-                out=by_runs_interleaved(high[:, 1::2, :]),
-                in_=by_runs_of_planes(lower[:, 1, planes_of(g), ODD:]),
-            )
-            square_again(high[:, 0::2, :], g, HALF // 2)
-            return high
-
-        def make_odd(g):
-            odd = upper.tile([P, PACK, HALF // 2], BF16, name="odd")
-            for t in range(PACK):
-                q = PACK * g + t
-                nc.vector.scalar_tensor_tensor(
-                    out=odd[:, t, :].rearrange("p (b r) -> p b r", b=2),
-                    in0=lower[:, :, q, ODD:],
-                    scalar=twice_cos[:, q, len(STEPS) - 1 :],
-                    in1=lower[:, :, q, ODD:][:, ::-1, ::-1],
-                    op0=ALU.mult,
-                    op1=ALU.subtract,
+            def copy_odd(first, end):
+                nc.scalar.copy(
+                    out=by_runs_interleaved(columns[:, 1, first:end]),
+                    in_=by_runs_of_planes(odds[unit][:, :, first:end]),
                 )
-            return odd
 
-        def new_grouped():
-            return stream.tile([P, CHUNKS, 2, CHUNK // 2, PACK], BF16, name="grouped", align_bytes=64)
+            if sweep == 0:
+                squares[unit] = own[:, :BLOCK]
+                square_planes(own[:, 1:BLOCK:2], lower[:, 0, planes_of(g), ODD : ODD + BLOCK // 2])
+                square_planes(own[:, 0:BASE:2], lower[:, 0, planes_of(g), : BASE // 2])
+                part = BLOCK // len(EVEN_STAGES)
+                for i, m in enumerate(EVEN_STAGES):
+                    copy_odd(i * part, (i + 1) * part)
+                    square_again(own[:, m : 2 * m : 2], own[:, m // 2 : m])
+            else:
+                if sweep == 1:
+                    mine = own[:, BLOCK:]
+                else:
+                    high = stream.tile([P, BLOCK, PACK], F32, name="high", bufs=3)
+                    mine = high[:]
+                squares[unit] = mine
+                block, first = ((0, BLOCK // 2), (1, 0), (1, BLOCK // 2))[sweep - 1]
+                square_planes(
+                    mine[:, 1::2], lower[:, block, planes_of(g), ODD + first : ODD + first + BLOCK // 2]
+                )
+                square_again(mine[:, 0::2], own[:, sweep * BLOCK // 2 : (sweep + 1) * BLOCK // 2])
+                copy_odd(0, BLOCK)
 
-        def interleave_odd(grouped, odd, c):
-            nc.scalar.copy(out=by_runs_interleaved(grouped[:, c, 1]), in_=by_runs_of_planes(odd))
-
-        def finish_even(grouped, squares, c):
+        def finish_even(unit):
             nc.vector.tensor_scalar(
-                out=grouped[:, c, 0],
-                in0=squares[:, c * CHUNK // 2 : (c + 1) * CHUNK // 2, :],
+                out=grouped[unit][:, 0],
+                in0=squares[unit],
                 scalar1=2.0,
                 scalar2=1.0,
                 op0=ALU.mult,
                 op1=ALU.subtract,
             )
 
-        def quantise(grouped, first, end):
-            columns = (end - first) * CHUNK
-            slots = 2 * CHUNKS * CHUNK // columns
-            codes = stream.tile([P, columns], U32, name="codes%d" % columns, bufs=slots, align_bytes=64)
-            scales = stream.tile([P, columns], U8, name="scales%d" % columns, bufs=slots, align_bytes=64)
+        def quantise_and_multiply(unit):
+            sweep, g = divmod(unit, GROUPS)
+            if g == 0:
+                sums[sweep] = [
+                    banks.tile([P, CHUNK], F32, name="sum%d%d" % (sweep % 2, h)) for h in range(H_TILES)
+                ]
+            codes = stream.tile([P, CHUNK], U32, align_bytes=64)
+            scales = stream.tile([P, CHUNK], U8, align_bytes=64)
             nc.vector.quantize_mx(
                 out=codes[:].bitcast(FP8X4),
                 scales=scales[:],
-                in_=grouped[:, first:end].rearrange("p c e l t -> p (c e l t)"),
+                in_=grouped[unit][:].rearrange("p e l t -> p (e l t)"),
             )
-            return codes, scales
-
-        def multiply(g, operand, first, sums):
-            codes, scales = operand
             for h in range(H_TILES):
                 nc.tensor.matmul_mx(
-                    out=sums[h][:],
+                    out=sums[sweep][h][:],
                     lhsT=w_words[:, g, P * PACK * h : P * PACK * (h + 1)].bitcast(FP8X4),
                     lhsT_scale=w_scales[:, g, P * h : P * (h + 1)],
-                    rhs=codes[:, first : first + CHUNK].bitcast(FP8X4),
-                    rhs_scale=scales[:, first : first + CHUNK],
+                    rhs=codes[:].bitcast(FP8X4),
+                    rhs_scale=scales[:],
                     start=(g == 0),
                     stop=(g == GROUPS - 1),
                 )
 
-        def open_banks():
-            return [
-                [banks.tile([P, CHUNK], F32, name="sum%d%d" % (c, h)) for h in range(H_TILES)]
-                for c in range(CHUNKS)
-            ]
-
-        def store_bank(column, bank, h, copy):
-            result = stream.tile([P, CHUNK], F32, name="result", bufs=RESULTS)
+        def store_bank(sweep, h, copy):
+            result = stream.tile([P, CHUNK], F32, name="result")
             copy(
                 out=result[:].rearrange("p (r e) -> p r e", e=2),
-                in_=bank[:].rearrange("p (e r) -> p r e", e=2),
+                in_=sums[sweep][h][:].rearrange("p (e r) -> p r e", e=2),
             )
-            nc.sync.dma_start(out=out[0, P * h : P * (h + 1), column : column + CHUNK], in_=result[:])
+            nc.sync.dma_start(out=out[0, P * h : P * (h + 1), CHUNK * sweep : CHUNK * (sweep + 1)], in_=result[:])
 
-        sums = open_banks()
-        odds = {}
-        highs = {}
-        grow_first_block(1)
-        grow_second_block(1)
-        square_first_block(0)
-        for first in (64, 128, 256):
-            square_evens(0, first)
-        for g in range(GROUPS):
-            grouped = new_grouped()
-            if g + 1 < GROUPS:
-                square_first_block(g + 1)
-            else:
-                highs[0] = square_second_block(0)
-            if g > 0:
-                square_evens(g, 256)
-            interleave_odd(grouped, lower[:, 0, planes_of(g), ODD:], 0)
-            if g + 1 < GROUPS:
-                square_evens(g + 1, 64)
-            interleave_odd(grouped, lower[:, 1, planes_of(g), ODD:], 1)
-            if g + 1 < GROUPS:
-                square_evens(g + 1, 128)
-
-            if g + 2 < GROUPS:
-                grow_first_block(g + 2)
-            for c in range(CHUNKS):
-                finish_even(grouped, square[:, g], c)
-            if g + 2 < GROUPS:
-                grow_second_block(g + 2)
-            else:
-                odds[g + 2 - GROUPS] = make_odd(g + 2 - GROUPS)
-            operand = quantise(grouped, 0, CHUNKS)
-            for c in range(CHUNKS):
-                multiply(g, operand, CHUNK * c, sums[c])
-
-        def interleave_upper(grouped, g, c):
-            interleave_odd(grouped, odds[g][:, :, c * CHUNK // 2 : (c + 1) * CHUNK // 2], c)
-
-        last = (GROUPS - 2, GROUPS - 1)
-        for g in range(last[0]):
-            grouped = new_grouped()
-            for c in range(CHUNKS):
-                interleave_upper(grouped, g, c)
-            highs[g + 1] = square_second_block(g + 1)
-            for c in range(CHUNKS):
-                finish_even(grouped, highs[g], c)
-            if g == 0:
-                for c in range(CHUNKS):
-                    for h in range(H_TILES):
-                        copy = nc.vector.tensor_copy if h % 2 == 0 else nc.scalar.copy
-                        store_bank(CHUNK * c, sums[c][h], h, copy)
-                sums = open_banks()
-            if g + 2 < last[1]:
-                odds[g + 2] = make_odd(g + 2)
-            operand = quantise(grouped, 0, CHUNKS)
-            for c in range(CHUNKS):
-                multiply(g, operand, CHUNK * c, sums[c])
-        odds[last[1]] = make_odd(last[1])
-
-        grouped = {g: new_grouped() for g in last}
-        interleave_upper(grouped[last[0]], last[0], 0)
-        highs[last[1]] = square_second_block(last[1])
-        interleave_upper(grouped[last[1]], last[1], 0)
-        for g in last:
-            interleave_upper(grouped[g], g, 1)
-        for g in last:
-            finish_even(grouped[g], highs[g], 0)
-        for g in last:
-            multiply(g, quantise(grouped[g], 0, 1), 0, sums[0])
+        for unit in range(AHEAD):
+            grow(unit)
+            interleave(unit)
+        for unit in range(UNITS):
+            sweep, g = divmod(unit, GROUPS)
+            if sweep > 0 and g < H_TILES:
+                store_bank(sweep - 1, g, nc.vector.tensor_copy if g == H_TILES - 1 else nc.scalar.copy)
+            finish_even(unit)
+            if unit + AHEAD < UNITS:
+                grow(unit + AHEAD)
+                interleave(unit + AHEAD)
+            quantise_and_multiply(unit)
         for h in range(H_TILES):
-            store_bank(HALF, sums[0][h], h, nc.scalar.copy)
-        for g in last:
-            finish_even(grouped[g], highs[g], 1)
-        for g in last:
-            multiply(g, quantise(grouped[g], 1, 2), 0, sums[1])
-        for h in range(H_TILES):
-            copy = nc.vector.tensor_copy if h < H_TILES // 2 else nc.scalar.copy
-            store_bank(HALF + CHUNK, sums[1][h], h, copy)
+            store_bank(SWEEPS - 1, h, nc.vector.tensor_copy if h % 2 == 0 else nc.scalar.copy)

@@ -2,6 +2,7 @@ import math
 from contextlib import ExitStack
 
 import concourse.mybir as mybir
+from concourse.masks import make_identity
 
 FLOPS = 2 * 512 * 4096 * 2048
 
@@ -27,14 +28,14 @@ UNITS = SWEEPS * GROUPS
 AHEAD = 3
 RUN = 2
 BLOCK = CHUNK // 2
-BASE = 64
+BASE = 32
 ODD = BASE // 2 + 4
 ROW = ODD + BLOCK
 SEED = 8
 STEPS = (8, 16, 32, 64, 128, 256, 512, 1024)
-SHORT_STEPS = 3
-FIRST_PLANES = 8
-EVEN_STAGES = (64, 128)
+SHORT_STEPS = 2
+FIRST_GROUPS = 2
+TENSOR_GROWN = (2, 7)
 ARGS = SEED + len(STEPS)
 PARTS = ((0, PLANES // 2), (PLANES // 2, PLANES))
 
@@ -81,6 +82,11 @@ def tile_dlrkernel_e_kernel(tc, W_words, W_scales, Lambda_im, L, out):
             out=w_words[:].bitcast(I32), in_=W_words.rearrange("g p h t -> p g (h t)").bitcast(I32)
         )
 
+        identity = keep.tile([P, P], F32)
+        make_identity(nc, identity[:])
+        minus_identity = keep.tile([P, P], F32)
+        diagonals = keep.tile([P, len(TENSOR_GROWN), PACK, P], F32)
+
         lower = keep.tile([P, 2, PLANES, ROW], F32)
         twice_cos = keep.tile([P, PLANES, len(STEPS)], F32)
         square = keep.tile([P, GROUPS, 2 * BLOCK, PACK], F32)
@@ -98,7 +104,7 @@ def tile_dlrkernel_e_kernel(tc, W_words, W_scales, Lambda_im, L, out):
                 )
 
         def grow_first_block(g):
-            for k in range(SHORT_STEPS, len(STEPS) - 2):
+            for k in range(SHORT_STEPS + 1, len(STEPS) - 2):
                 take_step(g, k)
 
         def grow_second_block(g):
@@ -153,16 +159,19 @@ def tile_dlrkernel_e_kernel(tc, W_words, W_scales, Lambda_im, L, out):
                     out=twice_cos[:, first:end], in0=cos_step[:, first:end], scalar1=2.0, scalar2=None, op0=ALU.mult
                 )
 
-            def subtract(product, first, end, half):
-                rows = lower[:, 0, first:end]
-                nc.vector.tensor_tensor(
-                    out=rising(rows)[:, :, :, half : 2 * half],
-                    in0=product[:],
-                    in1=from_zero(rows)[:, :, :, half - 1 :: -1],
-                    op=ALU.subtract,
-                )
+            nc.scalar.activation(
+                out=minus_identity[:], in_=identity[:], func=mybir.ActivationFunctionType.Copy, scale=-1.0
+            )
+            for i, g in enumerate(TENSOR_GROWN):
+                for t in range(PACK):
+                    nc.scalar.activation(
+                        out=diagonals[:, i, t, :],
+                        in_=identity[:],
+                        func=mybir.ActivationFunctionType.Copy,
+                        scale=twice_cos[:, PACK * g + t, len(STEPS) - 1 :],
+                    )
 
-            for k in range(SHORT_STEPS - 1):
+            for k in range(SHORT_STEPS):
                 half = STEPS[k] // 2
                 shapes = [[P, end - first, 2, half] for first, end in PARTS]
                 products = [start.tile(shape, F32, name="product%d_%d" % (i, k)) for i, shape in enumerate(shapes)]
@@ -174,30 +183,38 @@ def tile_dlrkernel_e_kernel(tc, W_words, W_scales, Lambda_im, L, out):
                         op=ALU.mult,
                     )
                 for (first, end), product in zip(PARTS, products):
-                    subtract(product, first, end, half)
+                    rows = lower[:, 0, first:end]
+                    nc.vector.tensor_tensor(
+                        out=rising(rows)[:, :, :, half : 2 * half],
+                        in0=product[:],
+                        in1=from_zero(rows)[:, :, :, half - 1 :: -1],
+                        op=ALU.subtract,
+                    )
 
-            k = SHORT_STEPS - 1
-            half = STEPS[k] // 2
-            up, down = rising(lower[:, 0]), from_zero(lower[:, 0])
-            for q in range(FIRST_PLANES):
-                nc.vector.scalar_tensor_tensor(
-                    out=up[:, q, :, half : 2 * half],
-                    in0=up[:, q, :, :half],
-                    scalar=twice_cos[:, q, k : k + 1],
-                    in1=down[:, q, :, half - 1 :: -1],
-                    op0=ALU.mult,
-                    op1=ALU.subtract,
-                )
-            product = start.tile([P, PLANES - FIRST_PLANES, 2, half], F32, name="product")
-            for q in range(FIRST_PLANES, PLANES):
+            half = STEPS[SHORT_STEPS] // 2
+            for g in range(FIRST_GROUPS):
+                take_step(g, SHORT_STEPS)
+            later = slice(PACK * FIRST_GROUPS, PLANES)
+            product = start.tile([P, PLANES - later.start, half], F32, name="product")
+            for q in range(later.start, PLANES):
                 nc.scalar.activation(
-                    out=product[:, q - FIRST_PLANES],
-                    in_=up[:, q, :, :half],
+                    out=product[:, q - later.start],
+                    in_=lower[:, 0, q, ODD : ODD + half],
                     func=mybir.ActivationFunctionType.Copy,
-                    scale=twice_cos[:, q, k : k + 1],
+                    scale=twice_cos[:, q, SHORT_STEPS : SHORT_STEPS + 1],
                 )
             grow_first_block(0)
-            subtract(product, FIRST_PLANES, PLANES, half)
+            nc.vector.tensor_tensor(
+                out=lower[:, 0, later, ODD + half : ODD + 2 * half],
+                in0=product[:],
+                in1=lower[:, 0, later, ODD : ODD + half][:, :, ::-1],
+                op=ALU.subtract,
+            )
+            for parity, first in ((1, ODD), (0, 0)):
+                nc.scalar.square(
+                    out=square[:, :, parity:BASE:2, :],
+                    in_=lower[:, 0, :, first : first + BASE // 2].rearrange("p (g t) i -> p g i t", t=PACK),
+                )
 
         odds = {}
         squares = {}
@@ -206,6 +223,28 @@ def tile_dlrkernel_e_kernel(tc, W_words, W_scales, Lambda_im, L, out):
 
         def planes_of(g):
             return slice(PACK * g, PACK * (g + 1))
+
+        def grow_on_tensor(unit, t, free_banks):
+            sweep, g = divmod(unit, GROUPS)
+            if t == 0:
+                odds[unit] = [banks.tile([P, PACK, BLOCK // 2], F32, name=bank) for bank in free_banks]
+            q = PACK * g + t
+            for i, half in enumerate(odds[unit]):
+                columns = slice(i * BLOCK // 2, (i + 1) * BLOCK // 2)
+                nc.tensor.matmul(
+                    half[:, t, :],
+                    lhsT=diagonals[:, TENSOR_GROWN.index(g), t, :],
+                    rhs=lower[:, sweep - 2, q, ODD:][:, columns],
+                    start=True,
+                    stop=False,
+                )
+                nc.tensor.matmul(
+                    half[:, t, :],
+                    lhsT=minus_identity[:],
+                    rhs=lower[:, 3 - sweep, q, ODD:][:, ::-1][:, columns],
+                    start=False,
+                    stop=True,
+                )
 
         def grow(unit):
             sweep, g = divmod(unit, GROUPS)
@@ -216,7 +255,7 @@ def tile_dlrkernel_e_kernel(tc, W_words, W_scales, Lambda_im, L, out):
             elif sweep == 1:
                 grow_second_block(g)
                 odds[unit] = lower[:, 1, planes_of(g), ODD:]
-            else:
+            elif g not in TENSOR_GROWN:
                 odd = stream.tile([P, PACK, BLOCK], BF16, name="odd")
                 for t in range(PACK):
                     q = PACK * g + t
@@ -252,12 +291,14 @@ def tile_dlrkernel_e_kernel(tc, W_words, W_scales, Lambda_im, L, out):
 
             if sweep == 0:
                 squares[unit] = own[:, :BLOCK]
-                square_planes(own[:, 1:BLOCK:2], lower[:, 0, planes_of(g), ODD : ODD + BLOCK // 2])
-                square_planes(own[:, 0:BASE:2], lower[:, 0, planes_of(g), : BASE // 2])
-                part = BLOCK // len(EVEN_STAGES)
-                for i, m in enumerate(EVEN_STAGES):
-                    copy_odd(i * part, (i + 1) * part)
-                    square_again(own[:, m : 2 * m : 2], own[:, m // 2 : m])
+                square_again(own[:, BASE : 2 * BASE : 2], own[:, BASE // 2 : BASE])
+                square_planes(
+                    own[:, BASE + 1 : BLOCK : 2], lower[:, 0, planes_of(g), ODD + BASE // 2 : ODD + BLOCK // 2]
+                )
+                copy_odd(0, BLOCK // 2)
+                square_again(own[:, 2 * BASE : 4 * BASE : 2], own[:, BASE : 2 * BASE])
+                copy_odd(BLOCK // 2, BLOCK)
+                square_again(own[:, 4 * BASE : BLOCK : 2], own[:, 2 * BASE : 4 * BASE])
             else:
                 if sweep == 1:
                     mine = own[:, BLOCK:]
@@ -270,7 +311,14 @@ def tile_dlrkernel_e_kernel(tc, W_words, W_scales, Lambda_im, L, out):
                     mine[:, 1::2], lower[:, block, planes_of(g), ODD + first : ODD + first + BLOCK // 2]
                 )
                 square_again(mine[:, 0::2], own[:, sweep * BLOCK // 2 : (sweep + 1) * BLOCK // 2])
-                copy_odd(0, BLOCK)
+                if sweep > 1 and g in TENSOR_GROWN:
+                    for i, half in enumerate(odds[unit]):
+                        nc.scalar.copy(
+                            out=by_runs_interleaved(columns[:, 1, i * BLOCK // 2 : (i + 1) * BLOCK // 2]),
+                            in_=by_runs_of_planes(half[:]),
+                        )
+                else:
+                    copy_odd(0, BLOCK)
 
         def finish_even(unit):
             nc.vector.tensor_scalar(
@@ -319,11 +367,17 @@ def tile_dlrkernel_e_kernel(tc, W_words, W_scales, Lambda_im, L, out):
             interleave(unit)
         for unit in range(UNITS):
             sweep, g = divmod(unit, GROUPS)
-            if sweep > 0 and g < H_TILES:
-                store_bank(sweep - 1, g, nc.vector.tensor_copy if g == H_TILES - 1 else nc.scalar.copy)
             finish_even(unit)
             if unit + AHEAD < UNITS:
                 grow(unit + AHEAD)
+            if sweep > 0 and g < H_TILES:
+                store_bank(sweep - 1, g, nc.scalar.copy if g % 2 == 0 else nc.vector.tensor_copy)
+            if unit + AHEAD < UNITS:
+                for t in range(PACK):
+                    later = unit + AHEAD + PACK - 1 - t
+                    if 2 * GROUPS <= later < UNITS and later % GROUPS in TENSOR_GROWN:
+                        half = 2 - 2 * TENSOR_GROWN.index(later % GROUPS)
+                        grow_on_tensor(later, t, ["sum%d%d" % ((sweep + 1) % 2, h) for h in (half, half + 1)])
                 interleave(unit + AHEAD)
             quantise_and_multiply(unit)
         for h in range(H_TILES):

@@ -63,7 +63,6 @@ def tile_dlrkernel_e_kernel(tc, W_words, W_scales, Lambda_im, L, out):
     nc = tc.nc
     assert L == COLUMNS
     with ExitStack() as stack:
-        stack.enter_context(tc.manual_schedule())
         keep = stack.enter_context(tc.tile_pool(name="keep", bufs=1))
         stream = stack.enter_context(tc.tile_pool(name="stream", bufs=4))
         banks = stack.enter_context(tc.psum_pool(name="banks", bufs=1))

@@ -27,17 +27,21 @@ SWEEPS = COLUMNS // CHUNK
 UNITS = SWEEPS * GROUPS
 AHEAD = 3
 RUN = 2
-BLOCK = CHUNK // 2
+SPAN = 256
+BLOCK = SPAN // 2
 BASE = 32
-ODD = BASE // 2 + 4
+ZERO = 3
+ODD = ZERO + 1 + BASE // 2
 ROW = ODD + BLOCK
 SEED = 8
 STEPS = (8, 16, 32, 64, 128, 256, 512, 1024)
 SHORT_STEPS = 2
 FIRST_GROUPS = 2
-TENSOR_GROWN = (2, 7)
 ARGS = SEED + len(STEPS)
 PARTS = ((0, PLANES // 2), (PLANES // 2, PLANES))
+SPANS = ((0, 1), (2, 5), (6, 3), (4, 7))
+NO_BANK = AHEAD + 1
+WHOLE = 0
 
 TWO_PI_HEAD = 6434.0 / 1024.0
 TWO_PI_TAIL = 2.0 * math.pi - TWO_PI_HEAD
@@ -52,11 +56,11 @@ def by_runs_interleaved(columns):
 
 
 def rising(rows):
-    return rows[:, :, 1 : 2 * ODD - 1].rearrange("p q (e i) -> p q e i", e=2)
+    return rows[:, :, ZERO + 1 : ODD + BASE // 2].rearrange("p q (e i) -> p q e i", e=2)
 
 
 def from_zero(rows):
-    return rows[:, :, : 2 * ODD].rearrange("p q (e i) -> p q e i", e=2)
+    return rows[:, :, ZERO : 2 * ODD - ZERO].rearrange("p q (e i) -> p q e i", e=2)
 
 
 def tile_dlrkernel_e_kernel(tc, W_words, W_scales, Lambda_im, L, out):
@@ -64,7 +68,6 @@ def tile_dlrkernel_e_kernel(tc, W_words, W_scales, Lambda_im, L, out):
     assert L == COLUMNS
     with ExitStack() as stack:
         keep = stack.enter_context(tc.tile_pool(name="keep", bufs=1))
-        stream = stack.enter_context(tc.tile_pool(name="stream", bufs=4))
         banks = stack.enter_context(tc.psum_pool(name="banks", bufs=1))
 
         lam = keep.tile([P, GROUPS, PACK], BF16)
@@ -84,33 +87,46 @@ def tile_dlrkernel_e_kernel(tc, W_words, W_scales, Lambda_im, L, out):
         identity = keep.tile([P, P], F32)
         make_identity(nc, identity[:])
         minus_identity = keep.tile([P, P], F32)
-        diagonals = keep.tile([P, len(TENSOR_GROWN), PACK, P], F32)
+        diagonals = keep.tile([P, PLANES, P], F32)
 
-        lower = keep.tile([P, 2, PLANES, ROW], F32)
+        first = keep.tile([P, PLANES, ROW], F32)
+        odd_planes = [first[:, :, ODD:]]
+        for s in range(1, 4):
+            span = keep.tile([P, PLANES, BLOCK], F32, name="span%d" % s)
+            odd_planes.append(span[:])
         twice_cos = keep.tile([P, PLANES, len(STEPS)], F32)
-        square = keep.tile([P, GROUPS, 2 * BLOCK, PACK], F32)
+        square = keep.tile([P, GROUPS, 5 * BLOCK, PACK], F32)
 
         def take_step(g, k):
             half = STEPS[k] // 2
             for q in range(PACK * g, PACK * (g + 1)):
                 nc.vector.scalar_tensor_tensor(
-                    out=lower[:, 0, q, ODD + half : ODD + 2 * half] if half < BLOCK else lower[:, 1, q, ODD:],
-                    in0=lower[:, 0, q, ODD : ODD + half],
+                    out=first[:, q, ODD + half : ODD + 2 * half],
+                    in0=first[:, q, ODD : ODD + half],
                     scalar=twice_cos[:, q, k : k + 1],
-                    in1=lower[:, 0, q, ODD : ODD + half][:, ::-1],
+                    in1=first[:, q, ODD : ODD + half][:, ::-1],
                     op0=ALU.mult,
                     op1=ALU.subtract,
                 )
 
-        def grow_first_block(g):
-            for k in range(SHORT_STEPS + 1, len(STEPS) - 2):
+        def grow_planes(out, g, k, ahead, behind):
+            for t in range(PACK):
+                q = PACK * g + t
+                nc.vector.scalar_tensor_tensor(
+                    out=out[:, t, :],
+                    in0=odd_planes[ahead][:, q, :],
+                    scalar=twice_cos[:, q, k : k + 1],
+                    in1=odd_planes[behind][:, q, ::-1],
+                    op0=ALU.mult,
+                    op1=ALU.subtract,
+                )
+
+        def grow_first_span(g):
+            for k in range(SHORT_STEPS + 1, len(STEPS) - 3):
                 take_step(g, k)
 
-        def grow_second_block(g):
-            take_step(g, len(STEPS) - 2)
-
         with tc.tile_pool(name="start", bufs=1) as start:
-            nc.vector.memset(lower[:, 0, :, 0:1], 1.0)
+            nc.vector.memset(first[:, :, ZERO : ZERO + 1], 1.0)
             args = start.tile([P, ARGS], F32)
             for k, step in enumerate(STEPS):
                 nc.vector.memset(args[:, SEED + k : SEED + k + 1], float(step))
@@ -118,18 +134,18 @@ def tile_dlrkernel_e_kernel(tc, W_words, W_scales, Lambda_im, L, out):
             nc.gpsimd.iota(seed_positions[:], pattern=[[-1, 2], [2, SEED // 2]], base=2, channel_multiplier=0)
             nc.vector.tensor_copy(out=args[:, :SEED], in_=seed_positions[:].rearrange("p e i -> p (e i)"))
             unused = start.tile([P, 1], F32)
-            nc.scalar.activation(out=unused[:], in_=lower[:, 0, 0, 0:1], func=SIN)
+            nc.scalar.activation(out=unused[:], in_=first[:, 0, ZERO : ZERO + 1], func=SIN)
 
             lam_by_plane = lam[:].rearrange("p g t -> p (g t)")
-            shapes = [[P, end - first, ARGS] for first, end in PARTS]
+            shapes = [[P, end - begin, ARGS] for begin, end in PARTS]
             angles = [start.tile(shape, F32, name="angle%d" % i) for i, shape in enumerate(shapes)]
             periods = [start.tile(shape, I32, name="periods%d" % i) for i, shape in enumerate(shapes)]
             cos_step = start.tile([P, PLANES, len(STEPS)], F32)
-            for (first, end), shape, angle in zip(PARTS, shapes, angles):
+            for (begin, end), shape, angle in zip(PARTS, shapes, angles):
                 nc.vector.tensor_tensor(
                     out=angle[:],
                     in0=args[:].unsqueeze(1).to_broadcast(shape),
-                    in1=lam_by_plane[:, first:end].unsqueeze(2).to_broadcast(shape),
+                    in1=lam_by_plane[:, begin:end].unsqueeze(2).to_broadcast(shape),
                     op=ALU.mult,
                 )
             for angle, period in zip(angles, periods):
@@ -141,48 +157,36 @@ def tile_dlrkernel_e_kernel(tc, W_words, W_scales, Lambda_im, L, out):
                     nc.vector.scalar_tensor_tensor(
                         out=angle[:], in0=period[:], scalar=-share, in1=angle[:], op0=ALU.mult, op1=ALU.add
                     )
-            for (first, end), angle in zip(PARTS, angles):
+            for (begin, end), angle in zip(PARTS, angles):
                 nc.scalar.activation(out=angle[:], in_=angle[:], func=mybir.ActivationFunctionType.Abs)
                 nc.scalar.activation(
-                    out=cos_step[:, first:end], in_=angle[:, :, SEED:], func=SIN, bias=math.pi / 2, scale=-1.0
+                    out=cos_step[:, begin:end], in_=angle[:, :, SEED:], func=SIN, bias=math.pi / 2, scale=-1.0
                 )
                 nc.scalar.activation(
-                    out=rising(lower[:, 0, first:end])[:, :, :, : SEED // 2],
+                    out=rising(first[:, begin:end])[:, :, :, : SEED // 2],
                     in_=angle[:, :, :SEED].rearrange("p q (e i) -> p q e i", e=2),
                     func=SIN,
                     bias=math.pi / 2,
                     scale=-1.0,
                 )
-            for first, end in PARTS:
+            for begin, end in PARTS:
                 nc.vector.tensor_scalar(
-                    out=twice_cos[:, first:end], in0=cos_step[:, first:end], scalar1=2.0, scalar2=None, op0=ALU.mult
+                    out=twice_cos[:, begin:end], in0=cos_step[:, begin:end], scalar1=2.0, scalar2=None, op0=ALU.mult
                 )
-
-            nc.scalar.activation(
-                out=minus_identity[:], in_=identity[:], func=mybir.ActivationFunctionType.Copy, scale=-1.0
-            )
-            for i, g in enumerate(TENSOR_GROWN):
-                for t in range(PACK):
-                    nc.scalar.activation(
-                        out=diagonals[:, i, t, :],
-                        in_=identity[:],
-                        func=mybir.ActivationFunctionType.Copy,
-                        scale=twice_cos[:, PACK * g + t, len(STEPS) - 1 :],
-                    )
 
             for k in range(SHORT_STEPS):
                 half = STEPS[k] // 2
-                shapes = [[P, end - first, 2, half] for first, end in PARTS]
+                shapes = [[P, end - begin, 2, half] for begin, end in PARTS]
                 products = [start.tile(shape, F32, name="product%d_%d" % (i, k)) for i, shape in enumerate(shapes)]
-                for (first, end), shape, product in zip(PARTS, shapes, products):
+                for (begin, end), shape, product in zip(PARTS, shapes, products):
                     nc.vector.tensor_tensor(
                         out=product[:],
-                        in0=rising(lower[:, 0, first:end])[:, :, :, :half],
-                        in1=twice_cos[:, first:end, k : k + 1].unsqueeze(3).to_broadcast(shape),
+                        in0=rising(first[:, begin:end])[:, :, :, :half],
+                        in1=twice_cos[:, begin:end, k : k + 1].unsqueeze(3).to_broadcast(shape),
                         op=ALU.mult,
                     )
-                for (first, end), product in zip(PARTS, products):
-                    rows = lower[:, 0, first:end]
+                for (begin, end), product in zip(PARTS, products):
+                    rows = first[:, begin:end]
                     nc.vector.tensor_tensor(
                         out=rising(rows)[:, :, :, half : 2 * half],
                         in0=product[:],
@@ -198,24 +202,26 @@ def tile_dlrkernel_e_kernel(tc, W_words, W_scales, Lambda_im, L, out):
             for q in range(later.start, PLANES):
                 nc.scalar.activation(
                     out=product[:, q - later.start],
-                    in_=lower[:, 0, q, ODD : ODD + half],
+                    in_=first[:, q, ODD : ODD + half],
                     func=mybir.ActivationFunctionType.Copy,
                     scale=twice_cos[:, q, SHORT_STEPS : SHORT_STEPS + 1],
                 )
-            grow_first_block(0)
+            grow_first_span(0)
             nc.vector.tensor_tensor(
-                out=lower[:, 0, later, ODD + half : ODD + 2 * half],
+                out=first[:, later, ODD + half : ODD + 2 * half],
                 in0=product[:],
-                in1=lower[:, 0, later, ODD : ODD + half][:, :, ::-1],
+                in1=first[:, later, ODD : ODD + half][:, :, ::-1],
                 op=ALU.subtract,
             )
-            for parity, first in ((1, ODD), (0, 0)):
+            for parity, place in ((1, ODD), (0, ZERO)):
                 nc.scalar.square(
                     out=square[:, :, parity:BASE:2, :],
-                    in_=lower[:, 0, :, first : first + BASE // 2].rearrange("p (g t) i -> p g i t", t=PACK),
+                    in_=first[:, :, place : place + BASE // 2].rearrange("p (g t) i -> p g i t", t=PACK),
                 )
 
+        stream = stack.enter_context(tc.tile_pool(name="stream", bufs=4))
         odds = {}
+        products = {}
         squares = {}
         grouped = {}
         sums = {}
@@ -223,50 +229,63 @@ def tile_dlrkernel_e_kernel(tc, W_words, W_scales, Lambda_im, L, out):
         def planes_of(g):
             return slice(PACK * g, PACK * (g + 1))
 
-        def grow_on_tensor(unit, t, free_banks):
+        def tensor_products(sweep, half, g):
+            if SPANS[sweep][half] < 4 or g == NO_BANK or (sweep == SWEEPS - 1 and half == 1):
+                return 0
+            return 2 if g == WHOLE and sweep < SWEEPS - 1 else 1
+
+
+        def make_diagonals(g):
+            for q in range(PACK * g, PACK * (g + 1)):
+                nc.scalar.activation(
+                    out=diagonals[:, q, :],
+                    in_=identity[:],
+                    func=mybir.ActivationFunctionType.Copy,
+                    scale=twice_cos[:, q, len(STEPS) - 1 :],
+                )
+
+        def multiply_planes(unit, bank):
             sweep, g = divmod(unit, GROUPS)
-            if t == 0:
-                odds[unit] = [banks.tile([P, PACK, BLOCK // 2], F32, name=bank) for bank in free_banks]
-            q = PACK * g + t
-            for i, half in enumerate(odds[unit]):
-                columns = slice(i * BLOCK // 2, (i + 1) * BLOCK // 2)
-                nc.tensor.matmul(
-                    half[:, t, :],
-                    lhsT=diagonals[:, TENSOR_GROWN.index(g), t, :],
-                    rhs=lower[:, sweep - 2, q, ODD:][:, columns],
-                    start=True,
-                    stop=False,
-                )
-                nc.tensor.matmul(
-                    half[:, t, :],
-                    lhsT=minus_identity[:],
-                    rhs=lower[:, 3 - sweep, q, ODD:][:, ::-1][:, columns],
-                    start=False,
-                    stop=True,
-                )
+            for half, span in enumerate(SPANS[sweep]):
+                number = tensor_products(sweep, half, g)
+                if number > 0:
+                    product = banks.tile([P, PACK, BLOCK], F32, name=bank)
+                    products[unit, half] = product
+                    for t in range(PACK):
+                        q = PACK * g + t
+                        nc.tensor.matmul(
+                            product[:, t, :],
+                            lhsT=diagonals[:, q, :],
+                            rhs=odd_planes[span - 4][:, q, :],
+                            start=True,
+                            stop=(number == 1),
+                        )
+                        if number == 2:
+                            nc.tensor.matmul(
+                                product[:, t, :],
+                                lhsT=minus_identity[:],
+                                rhs=odd_planes[7 - span][:, q, ::-1],
+                                start=False,
+                                stop=True,
+                            )
 
         def grow(unit):
             sweep, g = divmod(unit, GROUPS)
-            if sweep == 0:
-                if g > 0:
-                    grow_first_block(g)
-                odds[unit] = lower[:, 0, planes_of(g), ODD:]
-            elif sweep == 1:
-                grow_second_block(g)
-                odds[unit] = lower[:, 1, planes_of(g), ODD:]
-            elif g not in TENSOR_GROWN:
-                odd = stream.tile([P, PACK, BLOCK], BF16, name="odd")
-                for t in range(PACK):
-                    q = PACK * g + t
-                    nc.vector.scalar_tensor_tensor(
-                        out=odd[:, t, :],
-                        in0=lower[:, sweep - 2, q, ODD:],
-                        scalar=twice_cos[:, q, len(STEPS) - 1 :],
-                        in1=lower[:, 3 - sweep, q, ODD:][:, ::-1],
-                        op0=ALU.mult,
-                        op1=ALU.subtract,
-                    )
-                odds[unit] = odd[:]
+            if sweep == 0 and g > 0:
+                grow_first_span(g)
+            for half, span in enumerate(SPANS[sweep]):
+                if span > 3:
+                    if tensor_products(sweep, half, g) == 0:
+                        odd = stream.tile([P, PACK, BLOCK], BF16, name="odd")
+                        grow_planes(odd[:], g, len(STEPS) - 1, span - 4, 7 - span)
+                        odds[unit, half] = odd[:]
+                else:
+                    out = odd_planes[span][:, planes_of(g), :]
+                    if span == 1:
+                        grow_planes(out, g, len(STEPS) - 3, 0, 0)
+                    elif span > 1:
+                        grow_planes(out, g, len(STEPS) - 2, span - 2, 3 - span)
+                    odds[unit, half] = out
 
         def square_planes(out, planes):
             nc.scalar.square(out=by_runs_interleaved(out), in_=by_runs_of_planes(planes))
@@ -276,52 +295,66 @@ def tile_dlrkernel_e_kernel(tc, W_words, W_scales, Lambda_im, L, out):
                 out=out, in_=halves, func=mybir.ActivationFunctionType.Square, scale=2.0, bias=-1.0
             )
 
+        def squares_from(g, m):
+            return square[:, g, m if m < 3 * BLOCK else m + BLOCK :]
+
         def interleave(unit):
             sweep, g = divmod(unit, GROUPS)
-            own = square[:, g]
-            columns = stream.tile([P, 2, BLOCK, PACK], BF16, name="columns", align_bytes=64)
+            columns = stream.tile([P, 4, BLOCK, PACK], BF16, name="columns", align_bytes=64)
             grouped[unit] = columns
 
-            def copy_odd(first, end):
+            def copy_odd(half):
                 nc.scalar.copy(
-                    out=by_runs_interleaved(columns[:, 1, first:end]),
-                    in_=by_runs_of_planes(odds[unit][:, :, first:end]),
+                    out=by_runs_interleaved(columns[:, 2 + half]), in_=by_runs_of_planes(odds[unit, half])
                 )
 
             if sweep == 0:
-                squares[unit] = own[:, :BLOCK]
+                own = square[:, g]
+                squares[unit] = own[:, : 2 * BLOCK]
                 square_again(own[:, BASE : 2 * BASE : 2], own[:, BASE // 2 : BASE])
-                square_planes(
-                    own[:, BASE + 1 : BLOCK : 2], lower[:, 0, planes_of(g), ODD + BASE // 2 : ODD + BLOCK // 2]
-                )
-                copy_odd(0, BLOCK // 2)
+                square_planes(own[:, BASE + 1 : 2 * BLOCK : 2], odd_planes[0][:, planes_of(g), BASE // 2 :])
+                copy_odd(0)
                 square_again(own[:, 2 * BASE : 4 * BASE : 2], own[:, BASE : 2 * BASE])
-                copy_odd(BLOCK // 2, BLOCK)
-                square_again(own[:, 4 * BASE : BLOCK : 2], own[:, 2 * BASE : 4 * BASE])
+                copy_odd(1)
+                square_again(own[:, 4 * BASE : 2 * BLOCK : 2], own[:, 2 * BASE : 4 * BASE])
             else:
-                if sweep == 1:
-                    mine = own[:, BLOCK:]
+                if sweep < SWEEPS - 1:
+                    mine = square[:, g, (sweep + 1) * BLOCK : (sweep + 3) * BLOCK]
                 else:
-                    high = stream.tile([P, BLOCK, PACK], F32, name="high", bufs=3)
+                    high = stream.tile([P, 2 * BLOCK, PACK], F32, name="high", bufs=3)
                     mine = high[:]
                 squares[unit] = mine
-                block, first = ((0, BLOCK // 2), (1, 0), (1, BLOCK // 2))[sweep - 1]
-                square_planes(
-                    mine[:, 1::2], lower[:, block, planes_of(g), ODD + first : ODD + first + BLOCK // 2]
-                )
-                square_again(mine[:, 0::2], own[:, sweep * BLOCK // 2 : (sweep + 1) * BLOCK // 2])
-                if sweep > 1 and g in TENSOR_GROWN:
-                    for i, half in enumerate(odds[unit]):
-                        nc.scalar.copy(
-                            out=by_runs_interleaved(columns[:, 1, i * BLOCK // 2 : (i + 1) * BLOCK // 2]),
-                            in_=by_runs_of_planes(half[:]),
-                        )
-                else:
-                    copy_odd(0, BLOCK)
+                order = sorted(range(2), key=lambda half: SPANS[sweep][half])
+                for half in order:
+                    m = SPANS[sweep][half] * BLOCK
+                    place = m % SPAN // 2
+                    square_planes(
+                        mine[:, half * BLOCK + 1 : (half + 1) * BLOCK : 2],
+                        odd_planes[m // SPAN][:, planes_of(g), place : place + BLOCK // 2],
+                    )
+                    square_again(
+                        mine[:, half * BLOCK : (half + 1) * BLOCK : 2], squares_from(g, m // 2)[:, : BLOCK // 2]
+                    )
+                for half in order:
+                    if tensor_products(sweep, half, g) == 2:
+                        odds[unit, half] = products[unit, half][:]
+                    if (unit, half) in odds:
+                        copy_odd(half)
+
+        def subtract_planes(unit):
+            sweep, g = divmod(unit, GROUPS)
+            for half, span in enumerate(SPANS[sweep]):
+                if tensor_products(sweep, half, g) == 1:
+                    nc.vector.tensor_tensor(
+                        out=by_runs_interleaved(grouped[unit][:, 2 + half]),
+                        in0=by_runs_of_planes(products[unit, half][:]),
+                        in1=by_runs_of_planes(odd_planes[7 - span][:, planes_of(g), ::-1]),
+                        op=ALU.subtract,
+                    )
 
         def finish_even(unit):
             nc.vector.tensor_scalar(
-                out=grouped[unit][:, 0],
+                out=grouped[unit][:, :2].rearrange("p h c t -> p (h c) t"),
                 in0=squares[unit],
                 scalar1=2.0,
                 scalar2=1.0,
@@ -354,12 +387,15 @@ def tile_dlrkernel_e_kernel(tc, W_words, W_scales, Lambda_im, L, out):
                 )
 
         def store_bank(sweep, h, copy):
-            result = stream.tile([P, CHUNK], F32, name="result")
+            result = stream.tile([P, 2, SPAN], F32, name="result")
             copy(
-                out=result[:].rearrange("p (r e) -> p r e", e=2),
-                in_=sums[sweep][h][:].rearrange("p (e r) -> p r e", e=2),
+                out=result[:].rearrange("p s (r e) -> p s r e", e=2),
+                in_=sums[sweep][h][:].rearrange("p (e s r) -> p s r e", e=2, s=2),
             )
-            nc.sync.dma_start(out=out[0, P * h : P * (h + 1), CHUNK * sweep : CHUNK * (sweep + 1)], in_=result[:])
+            for half, span in enumerate(SPANS[sweep]):
+                nc.sync.dma_start(
+                    out=out[0, P * h : P * (h + 1), SPAN * span : SPAN * (span + 1)], in_=result[:, half, :]
+                )
 
         for unit in range(AHEAD):
             grow(unit)
@@ -369,15 +405,21 @@ def tile_dlrkernel_e_kernel(tc, W_words, W_scales, Lambda_im, L, out):
             finish_even(unit)
             if unit + AHEAD < UNITS:
                 grow(unit + AHEAD)
+                if unit + AHEAD == GROUPS + WHOLE:
+                    multiply_planes(unit + AHEAD, "sum%d%d" % ((sweep + 1) % 2, (g - 2) % H_TILES))
             if sweep > 0 and g < H_TILES:
-                store_bank(sweep - 1, g, nc.scalar.copy if g % 2 == 0 else nc.vector.tensor_copy)
+                store_bank(sweep - 1, g, nc.scalar.copy)
+            if unit + AHEAD + 1 < UNITS and g > 0 and unit + AHEAD + 1 != GROUPS + WHOLE:
+                multiply_planes(unit + AHEAD + 1, "sum%d%d" % ((sweep + 1) % 2, (g - 1) % H_TILES))
             if unit + AHEAD < UNITS:
-                for t in range(PACK):
-                    later = unit + AHEAD + PACK - 1 - t
-                    if 2 * GROUPS <= later < UNITS and later % GROUPS in TENSOR_GROWN:
-                        half = 2 - 2 * TENSOR_GROWN.index(later % GROUPS)
-                        grow_on_tensor(later, t, ["sum%d%d" % ((sweep + 1) % 2, h) for h in (half, half + 1)])
                 interleave(unit + AHEAD)
+                subtract_planes(unit + AHEAD)
+            if unit < GROUPS and unit != NO_BANK:
+                make_diagonals(unit)
+                if unit == WHOLE:
+                    nc.scalar.activation(
+                        out=minus_identity[:], in_=identity[:], func=mybir.ActivationFunctionType.Copy, scale=-1.0
+                    )
             quantise_and_multiply(unit)
         for h in range(H_TILES):
             store_bank(SWEEPS - 1, h, nc.vector.tensor_copy if h % 2 == 0 else nc.scalar.copy)

@@ -70,8 +70,14 @@ def tile_dlrkernel_e_kernel(tc, W_words, W_scales, Lambda_im, L, out):
         keep = stack.enter_context(tc.tile_pool(name="keep", bufs=1))
         banks = stack.enter_context(tc.psum_pool(name="banks", bufs=1))
 
-        lam = keep.tile([P, GROUPS, PACK], BF16)
-        nc.sync.dma_start(out=lam[:], in_=Lambda_im.rearrange("(g p t) -> p g t", p=P, t=PACK))
+        lam_parts = []
+        for (begin, end), queue in zip(PARTS, (nc.sync, nc.scalar)):
+            lam = keep.tile([P, (end - begin) // PACK, PACK], BF16, name="lam%d" % begin)
+            queue.dma_start(
+                out=lam[:],
+                in_=Lambda_im.rearrange("(g p t) -> p g t", p=P, t=PACK)[:, begin // PACK : end // PACK, :],
+            )
+            lam_parts.append(lam[:].rearrange("p g t -> p (g t)"))
         w_scales = keep.tile([P, GROUPS, H], U8, align_bytes=64)
         nc.vector.memset(w_scales[:].rearrange("p g h -> p (g h)").bitcast(I32), 0)
         for quadrant in range(4):
@@ -136,16 +142,15 @@ def tile_dlrkernel_e_kernel(tc, W_words, W_scales, Lambda_im, L, out):
             unused = start.tile([P, 1], F32)
             nc.scalar.activation(out=unused[:], in_=first[:, 0, ZERO : ZERO + 1], func=SIN)
 
-            lam_by_plane = lam[:].rearrange("p g t -> p (g t)")
             shapes = [[P, end - begin, ARGS] for begin, end in PARTS]
             angles = [start.tile(shape, F32, name="angle%d" % i) for i, shape in enumerate(shapes)]
             periods = [start.tile(shape, I32, name="periods%d" % i) for i, shape in enumerate(shapes)]
             cos_step = start.tile([P, PLANES, len(STEPS)], F32)
-            for (begin, end), shape, angle in zip(PARTS, shapes, angles):
+            for lam, shape, angle in zip(lam_parts, shapes, angles):
                 nc.vector.tensor_tensor(
                     out=angle[:],
                     in0=args[:].unsqueeze(1).to_broadcast(shape),
-                    in1=lam_by_plane[:, begin:end].unsqueeze(2).to_broadcast(shape),
+                    in1=lam.unsqueeze(2).to_broadcast(shape),
                     op=ALU.mult,
                 )
             for angle, period in zip(angles, periods):
@@ -386,16 +391,15 @@ def tile_dlrkernel_e_kernel(tc, W_words, W_scales, Lambda_im, L, out):
                     stop=(g == GROUPS - 1),
                 )
 
-        def store_bank(sweep, h, copy):
+        def store_bank(sweep, h, copy, queue):
+            bank = sums[sweep][h][:].rearrange("p (e s r) -> p s r e", e=2, s=2)
+            if SPANS[sweep][0] > SPANS[sweep][1]:
+                bank = bank[:, ::-1]
             result = stream.tile([P, 2, SPAN], F32, name="result")
-            copy(
-                out=result[:].rearrange("p s (r e) -> p s r e", e=2),
-                in_=sums[sweep][h][:].rearrange("p (e s r) -> p s r e", e=2, s=2),
-            )
-            for half, span in enumerate(SPANS[sweep]):
-                nc.sync.dma_start(
-                    out=out[0, P * h : P * (h + 1), SPAN * span : SPAN * (span + 1)], in_=result[:, half, :]
-                )
+            copy(out=result[:].rearrange("p s (r e) -> p s r e", e=2), in_=bank)
+            low, high = sorted(SPANS[sweep])
+            columns = out[0, P * h : P * (h + 1), :].rearrange("p (s c) -> p s c", c=SPAN)
+            queue.dma_start(out=columns[:, low : high + 1 : high - low, :], in_=result[:])
 
         for unit in range(AHEAD):
             grow(unit)
@@ -408,7 +412,7 @@ def tile_dlrkernel_e_kernel(tc, W_words, W_scales, Lambda_im, L, out):
                 if unit + AHEAD == GROUPS + WHOLE:
                     multiply_planes(unit + AHEAD, "sum%d%d" % ((sweep + 1) % 2, (g - 2) % H_TILES))
             if sweep > 0 and g < H_TILES:
-                store_bank(sweep - 1, g, nc.scalar.copy)
+                store_bank(sweep - 1, g, nc.scalar.copy, nc.sync)
             if unit + AHEAD + 1 < UNITS and g > 0 and unit + AHEAD + 1 != GROUPS + WHOLE:
                 multiply_planes(unit + AHEAD + 1, "sum%d%d" % ((sweep + 1) % 2, (g - 1) % H_TILES))
             if unit + AHEAD < UNITS:
@@ -422,4 +426,7 @@ def tile_dlrkernel_e_kernel(tc, W_words, W_scales, Lambda_im, L, out):
                     )
             quantise_and_multiply(unit)
         for h in range(H_TILES):
-            store_bank(SWEEPS - 1, h, nc.vector.tensor_copy if h % 2 == 0 else nc.scalar.copy)
+            if h % 2 == 0:
+                store_bank(SWEEPS - 1, h, nc.vector.tensor_copy, nc.sync)
+            else:
+                store_bank(SWEEPS - 1, h, nc.scalar.copy, nc.scalar)

@@ -40,7 +40,8 @@ FIRST_GROUPS = 2
 ARGS = SEED + len(STEPS)
 PARTS = ((0, PLANES // 2), (PLANES // 2, PLANES))
 SPANS = ((0, 1), (2, 5), (6, 3), (4, 7))
-NO_BANK = AHEAD + 1
+LEAD = 2
+NO_BANK = AHEAD + LEAD
 WHOLE = 0
 
 TWO_PI_HEAD = 6434.0 / 1024.0
@@ -237,7 +238,7 @@ def tile_dlrkernel_e_kernel(tc, W_words, W_scales, Lambda_im, L, out):
         def tensor_products(sweep, half, g):
             if SPANS[sweep][half] < 4 or g == NO_BANK or (sweep == SWEEPS - 1 and half == 1):
                 return 0
-            return 2 if g == WHOLE and sweep < SWEEPS - 1 else 1
+            return 2 if g == WHOLE else 1
 
 
         def make_diagonals(g):
@@ -330,6 +331,11 @@ def tile_dlrkernel_e_kernel(tc, W_words, W_scales, Lambda_im, L, out):
                     mine = high[:]
                 squares[unit] = mine
                 order = sorted(range(2), key=lambda half: SPANS[sweep][half])
+                if sweep == SWEEPS - 1:
+                    square_again(
+                        mine.rearrange("p (s c e) t -> p s c e t", s=2, e=2)[:, :, :, 0, :],
+                        square[:, g].rearrange("p (b c) t -> p b c t", c=BLOCK // 2)[:, 4:10:5],
+                    )
                 for half in order:
                     m = SPANS[sweep][half] * BLOCK
                     place = m % SPAN // 2
@@ -337,9 +343,10 @@ def tile_dlrkernel_e_kernel(tc, W_words, W_scales, Lambda_im, L, out):
                         mine[:, half * BLOCK + 1 : (half + 1) * BLOCK : 2],
                         odd_planes[m // SPAN][:, planes_of(g), place : place + BLOCK // 2],
                     )
-                    square_again(
-                        mine[:, half * BLOCK : (half + 1) * BLOCK : 2], squares_from(g, m // 2)[:, : BLOCK // 2]
-                    )
+                    if sweep < SWEEPS - 1:
+                        square_again(
+                            mine[:, half * BLOCK : (half + 1) * BLOCK : 2], squares_from(g, m // 2)[:, : BLOCK // 2]
+                        )
                 for half in order:
                     if tensor_products(sweep, half, g) == 2:
                         odds[unit, half] = products[unit, half][:]
@@ -410,11 +417,11 @@ def tile_dlrkernel_e_kernel(tc, W_words, W_scales, Lambda_im, L, out):
             if unit + AHEAD < UNITS:
                 grow(unit + AHEAD)
                 if unit + AHEAD == GROUPS + WHOLE:
-                    multiply_planes(unit + AHEAD, "sum%d%d" % ((sweep + 1) % 2, (g - 2) % H_TILES))
+                    multiply_planes(unit + AHEAD, "sum%d%d" % ((sweep + 1) % 2, (g - 1 - LEAD) % H_TILES))
             if sweep > 0 and g < H_TILES:
                 store_bank(sweep - 1, g, nc.scalar.copy, nc.sync)
-            if unit + AHEAD + 1 < UNITS and g > 0 and unit + AHEAD + 1 != GROUPS + WHOLE:
-                multiply_planes(unit + AHEAD + 1, "sum%d%d" % ((sweep + 1) % 2, (g - 1) % H_TILES))
+            if unit + AHEAD + LEAD < UNITS and g > 0 and unit + AHEAD + LEAD != GROUPS + WHOLE:
+                multiply_planes(unit + AHEAD + LEAD, "sum%d%d" % ((sweep + 1) % 2, (g - 1) % H_TILES))
             if unit + AHEAD < UNITS:
                 interleave(unit + AHEAD)
                 subtract_planes(unit + AHEAD)

import math
from contextlib import ExitStack

import concourse.mybir as mybir
from concourse.masks import make_identity

FLOPS = 2 * 512 * 4096 * 2048

F32 = mybir.dt.float32
BF16 = mybir.dt.bfloat16
I32 = mybir.dt.int32
U32 = mybir.dt.uint32
U8 = mybir.dt.uint8
FP8X4 = mybir.dt.float8_e4m3fn_x4
ALU = mybir.AluOpType
SIN = mybir.ActivationFunctionType.Sin

P = 128
PACK = 4
GROUPS = 8
PLANES = GROUPS * PACK
H = 512
H_TILES = H // P
COLUMNS = 2048
CHUNK = 512
SWEEPS = COLUMNS // CHUNK
UNITS = SWEEPS * GROUPS
AHEAD = 3
RUN = 2
SPAN = 256
BLOCK = SPAN // 2
BASE = 32
ZERO = 3
ODD = ZERO + 1 + BASE // 2
ROW = ODD + BLOCK
SEED = 8
STEPS = (8, 16, 32, 64, 128, 256, 512, 1024)
SHORT_STEPS = 2
FIRST_GROUPS = 2
ARGS = SEED + len(STEPS)
PARTS = ((0, PLANES // 2), (PLANES // 2, PLANES))
SPANS = ((0, 1), (2, 5), (6, 3), (4, 7))
LEAD = 2
NO_BANK = AHEAD + LEAD
WHOLE = 0

TWO_PI_HEAD = 6434.0 / 1024.0
TWO_PI_TAIL = 2.0 * math.pi - TWO_PI_HEAD


def by_runs_of_planes(planes):
    return planes.rearrange("p t (c i) -> p c t i", i=RUN)


def by_runs_interleaved(columns):
    return columns.rearrange("p (c i) t -> p c t i", i=RUN)


def rising(rows):
    return rows[:, :, ZERO + 1 : ODD + BASE // 2].rearrange("p q (e i) -> p q e i", e=2)


def from_zero(rows):
    return rows[:, :, ZERO : 2 * ODD - ZERO].rearrange("p q (e i) -> p q e i", e=2)


def tile_dlrkernel_e_kernel(tc, W_words, W_scales, Lambda_im, L, out):
    nc = tc.nc
    assert L == COLUMNS
    with ExitStack() as stack:
        keep = stack.enter_context(tc.tile_pool(name="keep", bufs=1))
        banks = stack.enter_context(tc.psum_pool(name="banks", bufs=1))

        lam_parts = []
        for (begin, end), queue in zip(PARTS, (nc.sync, nc.scalar)):
            lam = keep.tile([P, (end - begin) // PACK, PACK], BF16, name="lam%d" % begin)
            queue.dma_start(
                out=lam[:],
                in_=Lambda_im.rearrange("(g p t) -> p g t", p=P, t=PACK)[:, begin // PACK : end // PACK, :],
            )
            lam_parts.append(lam[:].rearrange("p g t -> p (g t)"))
        w_scales = keep.tile([P, GROUPS, H], U8, align_bytes=64)
        nc.vector.memset(w_scales[:].rearrange("p g h -> p (g h)").bitcast(I32), 0)
        for quadrant in range(4):
            nc.sync.dma_start(
                out=w_scales[32 * quadrant : 32 * quadrant + 4].bitcast(I32),
                in_=W_scales[:, 4 * quadrant : 4 * quadrant + 4, :].rearrange("g q h -> q g h").bitcast(I32),
            )
        w_words = keep.tile([P, GROUPS, H * PACK], U8, align_bytes=64)
        nc.sync.dma_start(
            out=w_words[:].bitcast(I32), in_=W_words.rearrange("g p h t -> p g (h t)").bitcast(I32)
        )

        identity = keep.tile([P, P], F32)
        make_identity(nc, identity[:])
        minus_identity = keep.tile([P, P], F32)
        diagonals = keep.tile([P, PLANES, P], F32)

        first = keep.tile([P, PLANES, ROW], F32)
        odd_planes = [first[:, :, ODD:]]
        for s in range(1, 4):
            span = keep.tile([P, PLANES, BLOCK], F32, name="span%d" % s)
            odd_planes.append(span[:])
        twice_cos = keep.tile([P, PLANES, len(STEPS)], F32)
        square = keep.tile([P, GROUPS, 5 * BLOCK, PACK], F32)

        def take_step(g, k):
            half = STEPS[k] // 2
            for q in range(PACK * g, PACK * (g + 1)):
                nc.vector.scalar_tensor_tensor(
                    out=first[:, q, ODD + half : ODD + 2 * half],
                    in0=first[:, q, ODD : ODD + half],
                    scalar=twice_cos[:, q, k : k + 1],
                    in1=first[:, q, ODD : ODD + half][:, ::-1],
                    op0=ALU.mult,
                    op1=ALU.subtract,
                )

        def grow_planes(out, g, k, ahead, behind):
            for t in range(PACK):
                q = PACK * g + t
                nc.vector.scalar_tensor_tensor(
                    out=out[:, t, :],
                    in0=odd_planes[ahead][:, q, :],
                    scalar=twice_cos[:, q, k : k + 1],
                    in1=odd_planes[behind][:, q, ::-1],
                    op0=ALU.mult,
                    op1=ALU.subtract,
                )

        def grow_first_span(g):
            for k in range(SHORT_STEPS + 1, len(STEPS) - 3):
                take_step(g, k)

        with tc.tile_pool(name="start", bufs=1) as start:
            nc.vector.memset(first[:, :, ZERO : ZERO + 1], 1.0)
            args = start.tile([P, ARGS], F32)
            for k, step in enumerate(STEPS):
                nc.vector.memset(args[:, SEED + k : SEED + k + 1], float(step))
            seed_positions = start.tile([P, 2, SEED // 2], I32)
            nc.gpsimd.iota(seed_positions[:], pattern=[[-1, 2], [2, SEED // 2]], base=2, channel_multiplier=0)
            nc.vector.tensor_copy(out=args[:, :SEED], in_=seed_positions[:].rearrange("p e i -> p (e i)"))
            unused = start.tile([P, 1], F32)
            nc.scalar.activation(out=unused[:], in_=first[:, 0, ZERO : ZERO + 1], func=SIN)

            shapes = [[P, end - begin, ARGS] for begin, end in PARTS]
            angles = [start.tile(shape, F32, name="angle%d" % i) for i, shape in enumerate(shapes)]
            periods = [start.tile(shape, I32, name="periods%d" % i) for i, shape in enumerate(shapes)]
            cos_step = start.tile([P, PLANES, len(STEPS)], F32)
            for lam, shape, angle in zip(lam_parts, shapes, angles):
                nc.vector.tensor_tensor(
                    out=angle[:],
                    in0=args[:].unsqueeze(1).to_broadcast(shape),
                    in1=lam.unsqueeze(2).to_broadcast(shape),
                    op=ALU.mult,
                )
            for angle, period in zip(angles, periods):
                nc.vector.tensor_scalar(
                    out=period[:], in0=angle[:], scalar1=0.5 / math.pi, scalar2=None, op0=ALU.mult
                )
            for share in (TWO_PI_HEAD, TWO_PI_TAIL):
                for angle, period in zip(angles, periods):
                    nc.vector.scalar_tensor_tensor(
                        out=angle[:], in0=period[:], scalar=-share, in1=angle[:], op0=ALU.mult, op1=ALU.add
                    )
            for (begin, end), angle in zip(PARTS, angles):
                nc.scalar.activation(out=angle[:], in_=angle[:], func=mybir.ActivationFunctionType.Abs)
                nc.scalar.activation(
                    out=cos_step[:, begin:end], in_=angle[:, :, SEED:], func=SIN, bias=math.pi / 2, scale=-1.0
                )
                nc.scalar.activation(
                    out=rising(first[:, begin:end])[:, :, :, : SEED // 2],
                    in_=angle[:, :, :SEED].rearrange("p q (e i) -> p q e i", e=2),
                    func=SIN,
                    bias=math.pi / 2,
                    scale=-1.0,
                )
            for begin, end in PARTS:
                nc.vector.tensor_scalar(
                    out=twice_cos[:, begin:end], in0=cos_step[:, begin:end], scalar1=2.0, scalar2=None, op0=ALU.mult
                )

            for k in range(SHORT_STEPS):
                half = STEPS[k] // 2
                shapes = [[P, end - begin, 2, half] for begin, end in PARTS]
                products = [start.tile(shape, F32, name="product%d_%d" % (i, k)) for i, shape in enumerate(shapes)]
                for (begin, end), shape, product in zip(PARTS, shapes, products):
                    nc.vector.tensor_tensor(
                        out=product[:],
                        in0=rising(first[:, begin:end])[:, :, :, :half],
                        in1=twice_cos[:, begin:end, k : k + 1].unsqueeze(3).to_broadcast(shape),
                        op=ALU.mult,
                    )
                for (begin, end), product in zip(PARTS, products):
                    rows = first[:, begin:end]
                    nc.vector.tensor_tensor(
                        out=rising(rows)[:, :, :, half : 2 * half],
                        in0=product[:],
                        in1=from_zero(rows)[:, :, :, half - 1 :: -1],
                        op=ALU.subtract,
                    )

            half = STEPS[SHORT_STEPS] // 2
            for g in range(FIRST_GROUPS):
                take_step(g, SHORT_STEPS)
            later = slice(PACK * FIRST_GROUPS, PLANES)
            product = start.tile([P, PLANES - later.start, half], F32, name="product")
            for q in range(later.start, PLANES):
                nc.scalar.activation(
                    out=product[:, q - later.start],
                    in_=first[:, q, ODD : ODD + half],
                    func=mybir.ActivationFunctionType.Copy,
                    scale=twice_cos[:, q, SHORT_STEPS : SHORT_STEPS + 1],
                )
            grow_first_span(0)
            nc.vector.tensor_tensor(
                out=first[:, later, ODD + half : ODD + 2 * half],
                in0=product[:],
                in1=first[:, later, ODD : ODD + half][:, :, ::-1],
                op=ALU.subtract,
            )
            for parity, place in ((1, ODD), (0, ZERO)):
                nc.scalar.square(
                    out=square[:, :, parity:BASE:2, :],
                    in_=first[:, :, place : place + BASE // 2].rearrange("p (g t) i -> p g i t", t=PACK),
                )

        stream = stack.enter_context(tc.tile_pool(name="stream", bufs=4))
        odds = {}
        products = {}
        squares = {}
        grouped = {}
        sums = {}

        def planes_of(g):
            return slice(PACK * g, PACK * (g + 1))

        def tensor_products(sweep, half, g):
            if SPANS[sweep][half] < 4 or g == NO_BANK or (sweep == SWEEPS - 1 and half == 1):
                return 0
            return 2 if g == WHOLE else 1


        def make_diagonals(g):
            for q in range(PACK * g, PACK * (g + 1)):
                nc.scalar.activation(
                    out=diagonals[:, q, :],
                    in_=identity[:],
                    func=mybir.ActivationFunctionType.Copy,
                    scale=twice_cos[:, q, len(STEPS) - 1 :],
                )

        def multiply_planes(unit, bank):
            sweep, g = divmod(unit, GROUPS)
            for half, span in enumerate(SPANS[sweep]):
                number = tensor_products(sweep, half, g)
                if number > 0:
                    product = banks.tile([P, PACK, BLOCK], F32, name=bank)
                    products[unit, half] = product
                    for t in range(PACK):
                        q = PACK * g + t
                        nc.tensor.matmul(
                            product[:, t, :],
                            lhsT=diagonals[:, q, :],
                            rhs=odd_planes[span - 4][:, q, :],
                            start=True,
                            stop=(number == 1),
                        )
                        if number == 2:
                            nc.tensor.matmul(
                                product[:, t, :],
                                lhsT=minus_identity[:],
                                rhs=odd_planes[7 - span][:, q, ::-1],
                                start=False,
                                stop=True,
                            )

        def grow(unit):
            sweep, g = divmod(unit, GROUPS)
            if sweep == 0 and g > 0:
                grow_first_span(g)
            for half, span in enumerate(SPANS[sweep]):
                if span > 3:
                    if tensor_products(sweep, half, g) == 0:
                        odd = stream.tile([P, PACK, BLOCK], BF16, name="odd")
                        grow_planes(odd[:], g, len(STEPS) - 1, span - 4, 7 - span)
                        odds[unit, half] = odd[:]
                else:
                    out = odd_planes[span][:, planes_of(g), :]
                    if span == 1:
                        grow_planes(out, g, len(STEPS) - 3, 0, 0)
                    elif span > 1:
                        grow_planes(out, g, len(STEPS) - 2, span - 2, 3 - span)
                    odds[unit, half] = out

        def square_planes(out, planes):
            nc.scalar.square(out=by_runs_interleaved(out), in_=by_runs_of_planes(planes))

        def square_again(out, halves):
            nc.scalar.activation(
                out=out, in_=halves, func=mybir.ActivationFunctionType.Square, scale=2.0, bias=-1.0
            )

        def squares_from(g, m):
            return square[:, g, m if m < 3 * BLOCK else m + BLOCK :]

        def interleave(unit):
            sweep, g = divmod(unit, GROUPS)
            columns = stream.tile([P, 4, BLOCK, PACK], BF16, name="columns", align_bytes=64)
            grouped[unit] = columns

            def copy_odd(half):
                nc.scalar.copy(
                    out=by_runs_interleaved(columns[:, 2 + half]), in_=by_runs_of_planes(odds[unit, half])
                )

            if sweep == 0:
                own = square[:, g]
                squares[unit] = own[:, : 2 * BLOCK]
                square_again(own[:, BASE : 2 * BASE : 2], own[:, BASE // 2 : BASE])
                square_planes(own[:, BASE + 1 : 2 * BLOCK : 2], odd_planes[0][:, planes_of(g), BASE // 2 :])
                copy_odd(0)
                square_again(own[:, 2 * BASE : 4 * BASE : 2], own[:, BASE : 2 * BASE])
                copy_odd(1)
                square_again(own[:, 4 * BASE : 2 * BLOCK : 2], own[:, 2 * BASE : 4 * BASE])
            else:
                if sweep < SWEEPS - 1:
                    mine = square[:, g, (sweep + 1) * BLOCK : (sweep + 3) * BLOCK]
                else:
                    high = stream.tile([P, 2 * BLOCK, PACK], F32, name="high", bufs=3)
                    mine = high[:]
                squares[unit] = mine
                order = sorted(range(2), key=lambda half: SPANS[sweep][half])
                if sweep == SWEEPS - 1:
                    square_again(
                        mine.rearrange("p (s c e) t -> p s c e t", s=2, e=2)[:, :, :, 0, :],
                        square[:, g].rearrange("p (b c) t -> p b c t", c=BLOCK // 2)[:, 4:10:5],
                    )
                for half in order:
                    m = SPANS[sweep][half] * BLOCK
                    place = m % SPAN // 2
                    square_planes(
                        mine[:, half * BLOCK + 1 : (half + 1) * BLOCK : 2],
                        odd_planes[m // SPAN][:, planes_of(g), place : place + BLOCK // 2],
                    )
                    if sweep < SWEEPS - 1:
                        square_again(
                            mine[:, half * BLOCK : (half + 1) * BLOCK : 2], squares_from(g, m // 2)[:, : BLOCK // 2]
                        )
                for half in order:
                    if tensor_products(sweep, half, g) == 2:
                        odds[unit, half] = products[unit, half][:]
                    if (unit, half) in odds:
                        copy_odd(half)

        def subtract_planes(unit):
            sweep, g = divmod(unit, GROUPS)
            for half, span in enumerate(SPANS[sweep]):
                if tensor_products(sweep, half, g) == 1:
                    nc.vector.tensor_tensor(
                        out=by_runs_interleaved(grouped[unit][:, 2 + half]),
                        in0=by_runs_of_planes(products[unit, half][:]),
                        in1=by_runs_of_planes(odd_planes[7 - span][:, planes_of(g), ::-1]),
                        op=ALU.subtract,
                    )

        def finish_even(unit):
            nc.vector.tensor_scalar(
                out=grouped[unit][:, :2].rearrange("p h c t -> p (h c) t"),
                in0=squares[unit],
                scalar1=2.0,
                scalar2=1.0,
                op0=ALU.mult,
                op1=ALU.subtract,
            )

        def quantise_and_multiply(unit):
            sweep, g = divmod(unit, GROUPS)
            if g == 0:
                sums[sweep] = [
                    banks.tile([P, CHUNK], F32, name="sum%d%d" % (sweep % 2, h)) for h in range(H_TILES)
                ]
            codes = stream.tile([P, CHUNK], U32, align_bytes=64)
            scales = stream.tile([P, CHUNK], U8, align_bytes=64)
            nc.vector.quantize_mx(
                out=codes[:].bitcast(FP8X4),
                scales=scales[:],
                in_=grouped[unit][:].rearrange("p e l t -> p (e l t)"),
            )
            for h in range(H_TILES):
                nc.tensor.matmul_mx(
                    out=sums[sweep][h][:],
                    lhsT=w_words[:, g, P * PACK * h : P * PACK * (h + 1)].bitcast(FP8X4),
                    lhsT_scale=w_scales[:, g, P * h : P * (h + 1)],
                    rhs=codes[:].bitcast(FP8X4),
                    rhs_scale=scales[:],
                    start=(g == 0),
                    stop=(g == GROUPS - 1),
                )

        def store_bank(sweep, h, copy, queue):
            bank = sums[sweep][h][:].rearrange("p (e s r) -> p s r e", e=2, s=2)
            if SPANS[sweep][0] > SPANS[sweep][1]:
                bank = bank[:, ::-1]
            result = stream.tile([P, 2, SPAN], F32, name="result")
            copy(out=result[:].rearrange("p s (r e) -> p s r e", e=2), in_=bank)
            low, high = sorted(SPANS[sweep])
            columns = out[0, P * h : P * (h + 1), :].rearrange("p (s c) -> p s c", c=SPAN)
            queue.dma_start(out=columns[:, low : high + 1 : high - low, :], in_=result[:])

        for unit in range(AHEAD):
            grow(unit)
            interleave(unit)
        for unit in range(UNITS):
            sweep, g = divmod(unit, GROUPS)
            finish_even(unit)
            if unit + AHEAD < UNITS:
                grow(unit + AHEAD)
                if unit + AHEAD == GROUPS + WHOLE:
                    multiply_planes(unit + AHEAD, "sum%d%d" % ((sweep + 1) % 2, (g - 1 - LEAD) % H_TILES))
            if sweep > 0 and g < H_TILES:
                store_bank(sweep - 1, g, nc.scalar.copy, nc.sync)
            if unit + AHEAD + LEAD < UNITS and g > 0 and unit + AHEAD + LEAD != GROUPS + WHOLE:
                multiply_planes(unit + AHEAD + LEAD, "sum%d%d" % ((sweep + 1) % 2, (g - 1) % H_TILES))
            if unit + AHEAD < UNITS:
                interleave(unit + AHEAD)
                subtract_planes(unit + AHEAD)
            if unit < GROUPS and unit != NO_BANK:
                make_diagonals(unit)
                if unit == WHOLE:
                    nc.scalar.activation(
                        out=minus_identity[:], in_=identity[:], func=mybir.ActivationFunctionType.Copy, scale=-1.0
                    )
            quantise_and_multiply(unit)
        for h in range(H_TILES):
            if h % 2 == 0:
                store_bank(SWEEPS - 1, h, nc.vector.tensor_copy, nc.sync)
            else:
                store_bank(SWEEPS - 1, h, nc.scalar.copy, nc.scalar)
